import numpy as np
import ml_dtypes


def mxq(x, axis, fmt="e4m3"):
    dtype, down = {"e4m3": (ml_dtypes.float8_e4m3fn, 7), "e5m2": (ml_dtypes.float8_e5m2, 14)}[fmt]
    v = np.moveaxis(np.asarray(x, np.float32).astype(ml_dtypes.bfloat16).astype(np.float64), axis, -1)
    blocks = v.reshape(v.shape[:-1] + (-1, 32))
    amax = np.abs(blocks).max(-1, keepdims=True)
    byte = np.maximum(np.where(amax > 0, np.frexp(amax)[1] - 1 + 127, 0) - down, 1)
    scale = np.exp2(byte - 127.0)
    codes = (blocks / scale).astype(np.float32).astype(dtype).astype(np.float64)
    return np.moveaxis((codes * scale).reshape(v.shape), -1, axis)


WIDE = False


def mx_kscale(k):
    if not WIDE:
        return np.ones(k)
    levels = np.array([10, -10, 5, -5, 0])
    a = np.random.permutation(np.resize(levels, k // 512 * 4)).reshape(k // 512, 4)
    idx = np.arange(k)
    return np.exp2(a[idx // 512, idx % 128 // 32])


BF16 = ml_dtypes.bfloat16


def bf(x):
    return np.asarray(x, np.float32).astype(BF16)


def f64(x):
    return np.asarray(x).astype(np.float64)


E2M1 = np.array([0.0, 0.5, 1.0, 1.5, 2.0, 3.0, 4.0, 6.0, -0.0, -0.5, -1.0, -1.5, -2.0, -3.0, -4.0, -6.0])


def pack_weight(w, fmt):
    k, n = w.shape
    w = f64(bf(w)).reshape(k // 32, 32, n)
    amax = np.abs(w).max(1)
    if fmt == "e4m3":
        byte = np.frexp(amax)[1] - 1 + 127 - 7
    else:
        mant, ex = np.frexp(amax / 6.0)
        byte = np.where(mant > 0.5, ex, ex - 1) + 127
    byte = np.clip(np.where(amax > 0, byte, 1), 1, 254)
    scaled = (w * np.exp2(127.0 - byte)[:, None, :]).reshape(k, n).astype(np.float32)
    by_word = np.ascontiguousarray(scaled.reshape(k // 512, 128, 4, n).transpose(0, 1, 3, 2))
    if fmt == "e4m3":
        words = by_word.astype(ml_dtypes.float8_e4m3fn).view(np.uint8)
    else:
        c = by_word.astype(ml_dtypes.float4_e2m1fn).view(np.uint8) & 0xF
        words = c[..., 0::2] | (c[..., 1::2] << 4)
    return np.ascontiguousarray(words), np.ascontiguousarray(byte.astype(np.uint8).reshape(k // 512, 16, n))


def unpack_weight(words, scales, fmt):
    g, p, n, _ = words.shape
    if fmt == "e4m3":
        vals = np.ascontiguousarray(words).view(ml_dtypes.float8_e4m3fn).astype(np.float64)
    else:
        nib = np.empty((g, p, n, 4), np.uint8)
        nib[..., 0::2] = words & 0xF
        nib[..., 1::2] = words >> 4
        vals = E2M1[nib]
    vals = vals * np.repeat(np.exp2(scales.astype(np.float64) - 127.0), 8, axis=1)[..., None]
    return vals.transpose(0, 1, 3, 2).reshape(g * 512, n)


B, P, D, DFF = 8, 64, 512, 1024


def sigmoid(v):
    return 1.0 / (1.0 + np.exp(-v))


def setup_inputs():
    s = mx_kscale(D)
    inp = {
        'Zi': bf(np.random.standard_normal((B, P, D)) * s),
        'Ci': bf(np.random.standard_normal((B, P, DFF))),
        'Mi': bf(np.random.standard_normal((B, P, DFF))),
        'Hi': bf(np.random.standard_normal((B, P, DFF))),
        'Ni': bf(np.random.uniform(0.5, 1.5, (B, P, DFF))),
        'm': bf(np.random.uniform(0.0, 1.0, (B, P, 1))),
    }
    for n in ('WI', 'WF', 'WO', 'WZ'):
        words, scales = pack_weight(np.random.standard_normal((DFF, DFF)) * 0.7 / np.sqrt(DFF), 'e4m3')
        inp[n + '_w_words'] = words
        inp[n + '_w_scales'] = scales
        inp[n + '_b'] = bf(np.random.standard_normal(DFF) * 0.3)
    for n in ('RI', 'RF', 'RO', 'RZ'):
        words, scales = pack_weight(np.random.standard_normal((D, DFF)) * 0.7 / np.sqrt(D) / s[:, None], 'e4m3')
        inp[n + '_w_words'] = words
        inp[n + '_w_scales'] = scales
        inp[n + '_b'] = bf(np.random.standard_normal(DFF) * 0.3)
    return inp


def reference(Zi, Ci, Mi, Hi, Ni, m,
              WI_w_words, WI_w_scales, WI_b, WF_w_words, WF_w_scales, WF_b,
              WO_w_words, WO_w_scales, WO_b, WZ_w_words, WZ_w_scales, WZ_b,
              RI_w_words, RI_w_scales, RI_b, RF_w_words, RF_w_scales, RF_b,
              RO_w_words, RO_w_scales, RO_b, RZ_w_words, RZ_w_scales, RZ_b):
    Zi, Ci, Mi, Hi, Ni, m = f64(Zi), f64(Ci), f64(Mi), f64(Hi), f64(Ni), f64(m)
    Wh = np.concatenate([unpack_weight(WI_w_words, WI_w_scales, 'e4m3'), unpack_weight(WF_w_words, WF_w_scales, 'e4m3'),
                         unpack_weight(WO_w_words, WO_w_scales, 'e4m3'), unpack_weight(WZ_w_words, WZ_w_scales, 'e4m3')], axis=1)
    Wz = np.concatenate([unpack_weight(RI_w_words, RI_w_scales, 'e4m3'), unpack_weight(RF_w_words, RF_w_scales, 'e4m3'),
                         unpack_weight(RO_w_words, RO_w_scales, 'e4m3'), unpack_weight(RZ_w_words, RZ_w_scales, 'e4m3')], axis=1)
    bias = np.concatenate([f64(WI_b) + f64(RI_b), f64(WF_b) + f64(RF_b), f64(WO_b) + f64(RO_b), f64(WZ_b) + f64(RZ_b)])
    gates = (mxq(Hi, 2, 'e4m3') @ Wh) + (mxq(Zi, 2, 'e4m3') @ Wz) + bias
    I_tilde, F_tilde, O_tilde, Z_tilde = np.split(gates, 4, axis=-1)

    M_t = np.maximum(F_tilde + Mi, I_tilde)
    I_t = np.exp(I_tilde - M_t)
    F_t = np.exp(F_tilde + Mi - M_t)
    O_t = sigmoid(O_tilde)
    N_t = F_t * Ni + I_t
    Z_t = np.tanh(Z_tilde)
    C_t = (Ci * F_t + Z_t * I_t) * m + (1.0 - m) * Ci
    H_t = O_t * (C_t / N_t) * m + (1.0 - m) * Hi
    return (C_t, M_t, H_t, N_t)

@@ -1,0 +1,298 @@
+from contextlib import ExitStack
+
+import concourse.mybir as mybir
+from concourse.masks import make_identity
+
+F32 = mybir.dt.float32
+BF16 = mybir.dt.bfloat16
+I32 = mybir.dt.int32
+U32 = mybir.dt.uint32
+U8 = mybir.dt.uint8
+FP8X4 = mybir.dt.float8_e4m3fn_x4
+ALU = mybir.AluOpType
+ACT = mybir.ActivationFunctionType
+
+P = 128
+TOKENS = 512
+TOKEN_TILES = TOKENS // P
+D = 512
+DFF = 1024
+K_PASS = 512
+PASSES = (DFF + D) // K_PASS
+CHUNK = 512
+CHUNKS = DFF // CHUNK
+UNITS = CHUNKS * TOKEN_TILES
+GATES = ("I", "F", "Z", "O")
+LN_GROUP = 2
+
+FLOPS = 2 * TOKENS * (DFF + D) * 4 * DFF
+
+
+def tile_customlstmcell_kernel(
+    tc, Zi, Ci, Mi, Hi, Ni, m,
+    WI_w_words, WI_w_scales, WI_b, WF_w_words, WF_w_scales, WF_b,
+    WO_w_words, WO_w_scales, WO_b, WZ_w_words, WZ_w_scales, WZ_b,
+    RI_w_words, RI_w_scales, RI_b, RF_w_words, RF_w_scales, RF_b,
+    RO_w_words, RO_w_scales, RO_b, RZ_w_words, RZ_w_scales, RZ_b,
+    out_0, out_1, out_2, out_3,
+):
+    nc = tc.nc
+    w_words = {"I": WI_w_words, "F": WF_w_words, "Z": WZ_w_words, "O": WO_w_words}
+    r_words = {"I": RI_w_words, "F": RF_w_words, "Z": RZ_w_words, "O": RO_w_words}
+    w_scales = {"I": WI_w_scales, "F": WF_w_scales, "Z": WZ_w_scales, "O": WO_w_scales}
+    r_scales = {"I": RI_w_scales, "F": RF_w_scales, "Z": RZ_w_scales, "O": RO_w_scales}
+    w_bias = {"I": WI_b, "F": WF_b, "Z": WZ_b, "O": WO_b}
+    r_bias = {"I": RI_b, "F": RF_b, "Z": RZ_b, "O": RO_b}
+
+    def by_token(ap):
+        return ap.flatten_outer_dims().rearrange("(p t) d -> p t d", t=TOKEN_TILES)
+
+    c_out, m_out, h_out, n_out = by_token(out_0), by_token(out_1), by_token(out_2), by_token(out_3)
+
+    with ExitStack() as ctx:
+        keep = ctx.enter_context(tc.tile_pool(name="keep", bufs=1))
+        work = ctx.enter_context(tc.tile_pool(name="work", bufs=2))
+        psum = ctx.enter_context(tc.psum_pool(name="psum", bufs=8))
+        ctx.enter_context(tc.manual_schedule())
+
+        hi_sb = keep.tile([P, TOKEN_TILES, DFF], BF16)
+        zi_sb = keep.tile([P, TOKEN_TILES, D], BF16)
+        mi_sb = keep.tile([P, TOKEN_TILES, DFF], BF16)
+        ni_sb = keep.tile([P, TOKEN_TILES, DFF], BF16)
+        ci_sb = keep.tile([P, TOKEN_TILES, DFF], BF16)
+        m_bf = keep.tile([P, TOKEN_TILES], BF16)
+        codes = {}
+        for gate in GATES:
+            gate_codes = keep.tile([P, PASSES, DFF], U32, align_bytes=64, name="codes_" + gate)
+            codes[gate] = gate_codes
+        planes = keep.tile([P, PASSES, DFF], U8, align_bytes=64)
+        x_codes = keep.tile([P, PASSES, TOKENS], U32, align_bytes=64)
+        x_scales = keep.tile([P, PASSES, TOKENS], U8, align_bytes=64)
+        ident = keep.tile([P, P], F32)
+        ones = keep.tile([P, P], BF16)
+        bias_rows = keep.tile([P, len(GATES), DFF], BF16)
+        bias_all = keep.tile([P, len(GATES), DFF], F32)
+        mi_bias = keep.tile([P, TOKEN_TILES, DFF], F32)
+        m_f32 = keep.tile([P, TOKEN_TILES], F32)
+        one_minus_m = keep.tile([P, TOKEN_TILES], F32)
+        half_m = keep.tile([P, TOKEN_TILES], F32)
+
+        nc.vector.memset(planes[:].bitcast(I32), 0)
+        nc.vector.memset(bias_rows[:], 0.0)
+        nc.vector.memset(ones[:], 1.0)
+        make_identity(nc, ident[:])
+
+        nc.scalar.dma_start(out=hi_sb[:], in_=by_token(Hi))
+        nc.scalar.dma_start(out=zi_sb[:], in_=by_token(Zi))
+        for i, gate in enumerate(GATES):
+            nc.scalar.dma_start(out=bias_rows[0:1, i, :], in_=w_bias[gate].unsqueeze(0))
+            nc.scalar.dma_start(out=bias_rows[1:2, i, :], in_=r_bias[gate].unsqueeze(0))
+        nc.scalar.dma_start(out=m_bf[:], in_=m.flatten_outer_dims().rearrange("(p t) o -> p (t o)", t=TOKEN_TILES))
+        nc.scalar.dma_start(out=mi_sb[:], in_=by_token(Mi))
+
+        for i, gate in enumerate(GATES):
+            for quadrant in range(4):
+                rows = slice(4 * quadrant, 4 * quadrant + 4)
+                first = 32 * quadrant + 4 * i
+                nc.sync.dma_start(
+                    out=planes[first : first + 4, 0:2, :].bitcast(I32),
+                    in_=w_scales[gate][:, rows, :].rearrange("g r n -> r g n").bitcast(I32),
+                )
+                nc.sync.dma_start(
+                    out=planes[first : first + 4, 2:3, :].bitcast(I32),
+                    in_=r_scales[gate][:, rows, :].rearrange("g r n -> r g n").bitcast(I32),
+                )
+
+        def load_codes(gate, chunk):
+            cols = slice(chunk * CHUNK, (chunk + 1) * CHUNK)
+            nc.sync.dma_start(
+                out=codes[gate][:, 0:2, cols].bitcast(I32),
+                in_=w_words[gate].rearrange("g p n t -> p g (n t)").bitcast(I32)[:, :, cols],
+            )
+            nc.sync.dma_start(
+                out=codes[gate][:, 2:3, cols].bitcast(I32),
+                in_=r_words[gate].rearrange("g p n t -> p g (n t)").bitcast(I32)[:, :, cols],
+            )
+
+        load_codes("I", 0)
+        load_codes("F", 0)
+        nc.sync.dma_start(out=ni_sb[:], in_=by_token(Ni))
+        load_codes("Z", 0)
+        load_codes("O", 0)
+        nc.sync.dma_start(out=ci_sb[:], in_=by_token(Ci))
+        for gate in GATES:
+            load_codes(gate, 1)
+
+        x_blocks = ((hi_sb, 0), (hi_sb, 1), (zi_sb, 0))
+        grouped = []
+        for c in range(PASSES):
+            grouped_c = keep.tile([P, TOKENS * 4], BF16, align_bytes=64, name="grouped%d" % c)
+            grouped.append(grouped_c)
+
+        def transpose_block(c):
+            x_sb, g = x_blocks[c]
+            x_words = x_sb[:].bitcast(F32)
+            out_words = grouped[c][:].bitcast(F32).rearrange("p (r u) -> p r u", u=2)
+            for half in range(2):
+                xt = psum.tile([P, 2, 2 * P], F32, tag="bank")
+                for u in range(2):
+                    for s in range(2):
+                        nc.tensor.transpose(
+                            xt[:, u, s * P : (s + 1) * P],
+                            x_words[:, 2 * half + s, 256 * g + u : 256 * (g + 1) : 2],
+                            ident[:],
+                        )
+                tokens = slice(half * 2 * P, (half + 1) * 2 * P)
+                if half == 0:
+                    nc.vector.tensor_copy(out=out_words[:, tokens, :], in_=xt[:].rearrange("p u r -> p r u"))
+                else:
+                    nc.scalar.copy(out=out_words[:, tokens, :], in_=xt[:].rearrange("p u r -> p r u"))
+
+        def quantise_block(c):
+            nc.vector.quantize_mx(
+                out=x_codes[:, c, :].bitcast(FP8X4), scales=x_scales[:, c, :], in_=grouped[c][:]
+            )
+
+        transpose_block(0)
+        transpose_block(1)
+        quantise_block(0)
+        transpose_block(2)
+        quantise_block(1)
+        quantise_block(2)
+
+        for i in range(len(GATES)):
+            for chunk in range(CHUNKS):
+                cols = slice(chunk * CHUNK, (chunk + 1) * CHUNK)
+                spread = psum.tile([P, CHUNK], F32, tag="bank")
+                nc.tensor.matmul(out=spread[:], lhsT=ones[:], rhs=bias_rows[:, i, cols], start=True, stop=True)
+                nc.scalar.copy(out=bias_all[:, i, cols], in_=spread[:])
+
+        nc.vector.tensor_copy(out=m_f32[:], in_=m_bf[:])
+        nc.vector.tensor_scalar(out=one_minus_m[:], in0=m_bf[:], scalar1=-1.0, scalar2=1.0, op0=ALU.mult, op1=ALU.add)
+        nc.vector.tensor_scalar(out=half_m[:], in0=m_bf[:], scalar1=0.5, scalar2=None, op0=ALU.mult)
+        for t in range(TOKEN_TILES):
+            nc.vector.tensor_tensor(
+                out=mi_bias[:, t, :], in0=mi_sb[:, t, :], in1=bias_all[:, GATES.index("F"), :], op=ALU.add
+            )
+
+        live = {}
+
+        def place(unit):
+            chunk, t = divmod(unit, TOKEN_TILES)
+            return t, slice(chunk * CHUNK, (chunk + 1) * CHUNK)
+
+        def gate_matmuls(unit):
+            t, cols = place(unit)
+            tokens = slice(t * P, (t + 1) * P)
+            for i, gate in enumerate(GATES):
+                acc = psum.tile([P, CHUNK], F32, tag="bank")
+                for c in range(PASSES):
+                    nc.tensor.matmul_mx(
+                        out=acc[:],
+                        lhsT=x_codes[:, c, tokens].bitcast(FP8X4),
+                        lhsT_scale=x_scales[:, c, tokens],
+                        rhs=codes[gate][:, c, cols].bitcast(FP8X4),
+                        rhs_scale=planes[4 * i : P, c, cols],
+                        start=(c == 0),
+                        stop=(c == PASSES - 1),
+                    )
+                live[gate, unit] = acc
+
+        def leave_psum(unit):
+            t, cols = place(unit)
+            i_pre = work.tile([P, CHUNK], F32, bufs=1)
+            f_pre = work.tile([P, CHUNK], F32, bufs=1)
+            m_t = work.tile([P, CHUNK], F32, bufs=3)
+            d = work.tile([P, CHUNK], F32)
+            z = work.tile([P, CHUNK], F32)
+            o = work.tile([P, CHUNK], F32)
+            nc.vector.tensor_tensor(out=i_pre[:], in0=live["I", unit][:], in1=bias_all[:, GATES.index("I"), cols], op=ALU.add)
+            nc.vector.tensor_tensor(out=f_pre[:], in0=live["F", unit][:], in1=mi_bias[:, t, cols], op=ALU.add)
+            nc.vector.tensor_tensor(out=d[:], in0=f_pre[:], in1=i_pre[:], op=ALU.subtract)
+            nc.vector.tensor_tensor(out=m_t[:], in0=f_pre[:], in1=i_pre[:], op=ALU.max)
+            nc.sync.dma_start(out=m_out[:, t, cols], in_=m_t[:])
+            nc.vector.tensor_tensor(out=z[:], in0=live["Z", unit][:], in1=bias_all[:, GATES.index("Z"), cols], op=ALU.add)
+            nc.vector.tensor_tensor(out=o[:], in0=live["O", unit][:], in1=bias_all[:, GATES.index("O"), cols], op=ALU.add)
+            live["d", unit], live["z", unit], live["o", unit] = d, z, o
+
+        def gate_functions(unit):
+            t, cols = place(unit)
+            d, z, o = live["d", unit], live["z", unit], live["o", unit]
+            e_i = work.tile([P, CHUNK], F32)
+            g = work.tile([P, CHUNK], F32)
+            nc.scalar.activation(out=e_i[:], in_=d[:], func=ACT.Exp, scale=-1.0)
+            nc.scalar.activation(out=d[:], in_=d[:], func=ACT.Relu, scale=-1.0)
+            nc.scalar.activation(out=d[:], in_=d[:], func=ACT.Exp, scale=-1.0)
+            nc.scalar.activation(
+                out=g[:], in_=d[:], func=ACT.Identity, scale=m_f32[:, t : t + 1], bias=one_minus_m[:, t : t + 1]
+            )
+            nc.scalar.activation(out=z[:], in_=z[:], func=ACT.Tanh)
+            nc.scalar.activation(out=o[:], in_=o[:], func=ACT.Tanh, scale=0.5)
+            live["e_i", unit], live["g", unit] = e_i, g
+
+        def normaliser(unit):
+            t, cols = place(unit)
+            n_t = work.tile([P, CHUNK], F32, bufs=3)
+            nc.vector.tensor_tensor(out=n_t[:], in0=live["d", unit][:], in1=ni_sb[:, t, cols], op=ALU.mult)
+            nc.vector.scalar_tensor_tensor(
+                out=n_t[:], in0=live["e_i", unit][:], scalar=1.0, in1=n_t[:], op0=ALU.min, op1=ALU.add
+            )
+            nc.sync.dma_start(out=n_out[:, t, cols], in_=n_t[:])
+            live["n_t", unit] = n_t
+
+        def cell(unit):
+            t, cols = place(unit)
+            z = live["z", unit]
+            kept = work.tile([P, CHUNK], F32, bufs=1)
+            c_t = work.tile([P, CHUNK], F32, bufs=3)
+            oc = work.tile([P, CHUNK], F32, bufs=3)
+            nc.vector.tensor_tensor(out=kept[:], in0=live["g", unit][:], in1=ci_sb[:, t, cols], op=ALU.mult)
+            nc.vector.scalar_tensor_tensor(
+                out=z[:], in0=live["e_i", unit][:], scalar=1.0, in1=z[:], op0=ALU.min, op1=ALU.mult
+            )
+            nc.vector.scalar_tensor_tensor(
+                out=c_t[:], in0=z[:], scalar=m_f32[:, t : t + 1], in1=kept[:], op0=ALU.mult, op1=ALU.add
+            )
+            nc.sync.dma_start(out=c_out[:, t, cols], in_=c_t[:])
+            nc.vector.scalar_tensor_tensor(
+                out=oc[:], in0=live["o", unit][:], scalar=1.0, in1=c_t[:], op0=ALU.add, op1=ALU.mult
+            )
+            live["oc", unit] = oc
+
+        def reciprocals(units):
+            for unit in units:
+                r = work.tile([P, CHUNK], F32, bufs=2 * LN_GROUP)
+                nc.scalar.activation(out=r[:], in_=live["n_t", unit][:], func=ACT.Ln)
+                live["r", unit] = r
+            for unit in units:
+                nc.scalar.activation(out=live["r", unit][:], in_=live["r", unit][:], func=ACT.Exp, scale=-1.0)
+
+        def hidden(unit):
+            t, cols = place(unit)
+            r = live["r", unit]
+            nc.vector.scalar_tensor_tensor(
+                out=r[:], in0=live["oc", unit][:], scalar=half_m[:, t : t + 1], in1=r[:], op0=ALU.mult, op1=ALU.mult
+            )
+            nc.vector.scalar_tensor_tensor(
+                out=r[:], in0=hi_sb[:, t, cols], scalar=one_minus_m[:, t : t + 1], in1=r[:], op0=ALU.mult, op1=ALU.add
+            )
+            nc.sync.dma_start(out=h_out[:, t, cols], in_=r[:])
+
+        gate_matmuls(0)
+        gate_matmuls(1)
+        for step in range(UNITS + 2):
+            if step < UNITS:
+                leave_psum(step)
+                if step + 2 < UNITS:
+                    gate_matmuls(step + 2)
+                gate_functions(step)
+            done = step - 1
+            if 0 <= done < UNITS:
+                normaliser(done)
+                if done % LN_GROUP == LN_GROUP - 1:
+                    reciprocals(range(done - LN_GROUP + 1, done + 1))
+                cell(done)
+            ready = step - 2
+            if ready >= 0 and ready % LN_GROUP == LN_GROUP - 1:
+                for unit in range(ready - LN_GROUP + 1, ready + 1):
+                    hidden(unit)

@@ -22,8 +22,15 @@ PASSES = (DFF + D) // K_PASS
 CHUNK = 512
 CHUNKS = DFF // CHUNK
 UNITS = CHUNKS * TOKEN_TILES
+COLUMN_TILES = DFF // P
 GATES = ("I", "F", "Z", "O")
-LN_GROUP = 2
+TANH_GATES = ("Z", "O")
+TANH_GROUPS = len(TANH_GATES) * COLUMN_TILES
+GROUPS_PER_CHUNK = TANH_GROUPS // CHUNKS
+TANH_GROUPS_PER_STEP = TANH_GROUPS // UNITS
+LN_GROUP = 4
+CELL_LAG = GROUPS_PER_CHUNK // TANH_GROUPS_PER_STEP
+RECIPROCAL_LAG = CELL_LAG - 1
 
 FLOPS = 2 * TOKENS * (DFF + D) * 4 * DFF
 
@@ -51,8 +58,7 @@ def tile_customlstmcell_kernel(
 
     with ExitStack() as ctx:
         keep = ctx.enter_context(tc.tile_pool(name="keep", bufs=1))
-        work = ctx.enter_context(tc.tile_pool(name="work", bufs=2))
-        psum = ctx.enter_context(tc.psum_pool(name="psum", bufs=8))
+        psum = ctx.enter_context(tc.psum_pool(name="psum", bufs=2))
         ctx.enter_context(tc.manual_schedule())
 
         hi_sb = keep.tile([P, TOKEN_TILES, DFF], BF16)
@@ -65,43 +71,30 @@ def tile_customlstmcell_kernel(
         for gate in GATES:
             gate_codes = keep.tile([P, PASSES, DFF], U32, align_bytes=64, name="codes_" + gate)
             codes[gate] = gate_codes
-        planes = keep.tile([P, PASSES, DFF], U8, align_bytes=64)
+        planes = {}
+        plane_offset = {}
+        for mates in (("I", "F"), TANH_GATES):
+            shared = keep.tile([P, PASSES, DFF], U8, align_bytes=64, name="planes_" + mates[0] + mates[1])
+            for k, gate in enumerate(mates):
+                planes[gate] = shared
+                plane_offset[gate] = 4 * k
         x_codes = keep.tile([P, PASSES, TOKENS], U32, align_bytes=64)
         x_scales = keep.tile([P, PASSES, TOKENS], U8, align_bytes=64)
         ident = keep.tile([P, P], F32)
         ones = keep.tile([P, P], BF16)
-        bias_rows = keep.tile([P, len(GATES), DFF], BF16)
-        bias_all = keep.tile([P, len(GATES), DFF], F32)
+        bias_all = keep.tile([P, 2, DFF], F32)
+        tanh_bias = keep.tile([P, len(TANH_GATES), COLUMN_TILES], F32)
         mi_bias = keep.tile([P, TOKEN_TILES, DFF], F32)
+        tanh_w_rows = keep.tile([P, P], BF16)
+        tanh_r_rows = keep.tile([P, P], BF16)
+        tanh_rows = keep.tile([P, P], F32)
         m_f32 = keep.tile([P, TOKEN_TILES], F32)
         one_minus_m = keep.tile([P, TOKEN_TILES], F32)
         half_m = keep.tile([P, TOKEN_TILES], F32)
 
-        nc.vector.memset(planes[:].bitcast(I32), 0)
-        nc.vector.memset(bias_rows[:], 0.0)
-        nc.vector.memset(ones[:], 1.0)
-        make_identity(nc, ident[:])
-
-        nc.scalar.dma_start(out=hi_sb[:], in_=by_token(Hi))
-        nc.scalar.dma_start(out=zi_sb[:], in_=by_token(Zi))
-        for i, gate in enumerate(GATES):
-            nc.scalar.dma_start(out=bias_rows[0:1, i, :], in_=w_bias[gate].unsqueeze(0))
-            nc.scalar.dma_start(out=bias_rows[1:2, i, :], in_=r_bias[gate].unsqueeze(0))
-        nc.scalar.dma_start(out=m_bf[:], in_=m.flatten_outer_dims().rearrange("(p t) o -> p (t o)", t=TOKEN_TILES))
-        nc.scalar.dma_start(out=mi_sb[:], in_=by_token(Mi))
-
-        for i, gate in enumerate(GATES):
-            for quadrant in range(4):
-                rows = slice(4 * quadrant, 4 * quadrant + 4)
-                first = 32 * quadrant + 4 * i
-                nc.sync.dma_start(
-                    out=planes[first : first + 4, 0:2, :].bitcast(I32),
-                    in_=w_scales[gate][:, rows, :].rearrange("g r n -> r g n").bitcast(I32),
-                )
-                nc.sync.dma_start(
-                    out=planes[first : first + 4, 2:3, :].bitcast(I32),
-                    in_=r_scales[gate][:, rows, :].rearrange("g r n -> r g n").bitcast(I32),
-                )
+        def place(unit):
+            chunk, t = divmod(unit, TOKEN_TILES)
+            return t, slice(chunk * CHUNK, (chunk + 1) * CHUNK)
 
         def load_codes(gate, chunk):
             cols = slice(chunk * CHUNK, (chunk + 1) * CHUNK)
@@ -114,89 +107,175 @@ def tile_customlstmcell_kernel(
                 in_=r_words[gate].rearrange("g p n t -> p g (n t)").bitcast(I32)[:, :, cols],
             )
 
-        load_codes("I", 0)
-        load_codes("F", 0)
-        nc.sync.dma_start(out=ni_sb[:], in_=by_token(Ni))
-        load_codes("Z", 0)
-        load_codes("O", 0)
-        nc.sync.dma_start(out=ci_sb[:], in_=by_token(Ci))
-        for gate in GATES:
-            load_codes(gate, 1)
+        with tc.tile_pool(name="prep", bufs=1) as prep:
+            bias_rows = prep.tile([P, 2, DFF], BF16)
+            grouped = []
+            for c in range(PASSES):
+                grouped_c = prep.tile([P, TOKENS * 4], BF16, align_bytes=64, name="grouped%d" % c)
+                grouped.append(grouped_c)
 
-        x_blocks = ((hi_sb, 0), (hi_sb, 1), (zi_sb, 0))
-        grouped = []
-        for c in range(PASSES):
-            grouped_c = keep.tile([P, TOKENS * 4], BF16, align_bytes=64, name="grouped%d" % c)
-            grouped.append(grouped_c)
+            nc.vector.memset(planes["I"][:].bitcast(I32), 0)
+            nc.vector.memset(planes["Z"][:].bitcast(I32), 0)
+            nc.vector.memset(bias_rows[:], 0.0)
+            nc.vector.memset(ones[:], 1.0)
+            nc.vector.memset(tanh_w_rows[:], 0.0)
+            nc.vector.memset(tanh_r_rows[:], 0.0)
+            make_identity(nc, ident[:])
 
-        def transpose_block(c):
-            x_sb, g = x_blocks[c]
-            x_words = x_sb[:].bitcast(F32)
-            out_words = grouped[c][:].bitcast(F32).rearrange("p (r u) -> p r u", u=2)
-            for half in range(2):
-                xt = psum.tile([P, 2, 2 * P], F32, tag="bank")
-                for u in range(2):
-                    for s in range(2):
-                        nc.tensor.transpose(
-                            xt[:, u, s * P : (s + 1) * P],
-                            x_words[:, 2 * half + s, 256 * g + u : 256 * (g + 1) : 2],
-                            ident[:],
-                        )
-                tokens = slice(half * 2 * P, (half + 1) * 2 * P)
-                if half == 0:
-                    nc.vector.tensor_copy(out=out_words[:, tokens, :], in_=xt[:].rearrange("p u r -> p r u"))
-                else:
-                    nc.scalar.copy(out=out_words[:, tokens, :], in_=xt[:].rearrange("p u r -> p r u"))
+            def load_scales(gate):
+                for quadrant in range(4):
+                    rows = slice(4 * quadrant, 4 * quadrant + 4)
+                    first = 32 * quadrant + plane_offset[gate]
+                    nc.sync.dma_start(
+                        out=planes[gate][first : first + 4, 0:2, :].bitcast(I32),
+                        in_=w_scales[gate][:, rows, :].rearrange("g r n -> r g n").bitcast(I32),
+                    )
+                    nc.sync.dma_start(
+                        out=planes[gate][first : first + 4, 2:3, :].bitcast(I32),
+                        in_=r_scales[gate][:, rows, :].rearrange("g r n -> r g n").bitcast(I32),
+                    )
 
-        def quantise_block(c):
-            nc.vector.quantize_mx(
-                out=x_codes[:, c, :].bitcast(FP8X4), scales=x_scales[:, c, :], in_=grouped[c][:]
+            nc.scalar.dma_start(out=hi_sb[:], in_=by_token(Hi))
+            nc.scalar.dma_start(out=zi_sb[:], in_=by_token(Zi))
+            nc.sync.dma_start(
+                out=m_bf[:], in_=m.flatten_outer_dims().rearrange("(p t) o -> p (t o)", t=TOKEN_TILES)
             )
+            for gate in ("F", "I"):
+                nc.sync.dma_start(out=bias_rows[0:1, GATES.index(gate), :], in_=w_bias[gate].unsqueeze(0))
+                nc.sync.dma_start(out=bias_rows[1:2, GATES.index(gate), :], in_=r_bias[gate].unsqueeze(0))
+            nc.sync.dma_start(out=mi_sb[:], in_=by_token(Mi))
+            for gate in ("I", "F"):
+                load_scales(gate)
+            for gate in ("I", "F"):
+                load_codes(gate, 0)
+            nc.sync.dma_start(out=ni_sb[:], in_=by_token(Ni))
+            for i, gate in enumerate(TANH_GATES):
+                rows = slice(i * COLUMN_TILES, (i + 1) * COLUMN_TILES)
+                nc.sync.dma_start(out=tanh_w_rows[rows, :], in_=w_bias[gate].rearrange("(i n) -> i n", n=P))
+                nc.sync.dma_start(out=tanh_r_rows[rows, :], in_=r_bias[gate].rearrange("(i n) -> i n", n=P))
+            for gate in TANH_GATES:
+                load_scales(gate)
+            for gate in TANH_GATES:
+                load_codes(gate, 0)
+            nc.sync.dma_start(out=ci_sb[:], in_=by_token(Ci))
 
-        transpose_block(0)
-        transpose_block(1)
-        quantise_block(0)
-        transpose_block(2)
-        quantise_block(1)
-        quantise_block(2)
+            x_blocks = ((hi_sb, 0), (hi_sb, 1), (zi_sb, 0))
 
-        for i in range(len(GATES)):
+            def transpose_block(c):
+                x_sb, g = x_blocks[c]
+                x_words = x_sb[:].bitcast(F32)
+                out_words = grouped[c][:].bitcast(F32).rearrange("p (r u) -> p r u", u=2)
+                for half in range(2):
+                    xt = psum.tile([P, 2, 2 * P], F32, tag="if", bufs=4)
+                    for u in range(2):
+                        for s in range(2):
+                            nc.tensor.transpose(
+                                xt[:, u, s * P : (s + 1) * P],
+                                x_words[:, 2 * half + s, 256 * g + u : 256 * (g + 1) : 2],
+                                ident[:],
+                            )
+                    tokens = slice(half * 2 * P, (half + 1) * 2 * P)
+                    if half == 0:
+                        nc.vector.tensor_copy(out=out_words[:, tokens, :], in_=xt[:].rearrange("p u r -> p r u"))
+                    else:
+                        nc.scalar.copy(out=out_words[:, tokens, :], in_=xt[:].rearrange("p u r -> p r u"))
+
+            def quantise_block(c):
+                nc.vector.quantize_mx(
+                    out=x_codes[:, c, :].bitcast(FP8X4), scales=x_scales[:, c, :], in_=grouped[c][:]
+                )
+
+            transpose_block(0)
+            transpose_block(1)
+            quantise_block(0)
+            transpose_block(2)
+            quantise_block(1)
+            quantise_block(2)
+
             for chunk in range(CHUNKS):
                 cols = slice(chunk * CHUNK, (chunk + 1) * CHUNK)
-                spread = psum.tile([P, CHUNK], F32, tag="bank")
-                nc.tensor.matmul(out=spread[:], lhsT=ones[:], rhs=bias_rows[:, i, cols], start=True, stop=True)
-                nc.scalar.copy(out=bias_all[:, i, cols], in_=spread[:])
+                for gate in ("F", "I"):
+                    i = GATES.index(gate)
+                    spread = psum.tile([P, CHUNK], F32, tag="tanh_in")
+                    nc.tensor.matmul(out=spread[:], lhsT=ones[:], rhs=bias_rows[:, i, cols], start=True, stop=True)
+                    nc.scalar.copy(out=bias_all[:, i, cols], in_=spread[:])
 
-        nc.vector.tensor_copy(out=m_f32[:], in_=m_bf[:])
-        nc.vector.tensor_scalar(out=one_minus_m[:], in0=m_bf[:], scalar1=-1.0, scalar2=1.0, op0=ALU.mult, op1=ALU.add)
-        nc.vector.tensor_scalar(out=half_m[:], in0=m_bf[:], scalar1=0.5, scalar2=None, op0=ALU.mult)
-        for t in range(TOKEN_TILES):
-            nc.vector.tensor_tensor(
-                out=mi_bias[:, t, :], in0=mi_sb[:, t, :], in1=bias_all[:, GATES.index("F"), :], op=ALU.add
+            nc.vector.tensor_copy(out=m_f32[:], in_=m_bf[:])
+            nc.vector.tensor_scalar(
+                out=one_minus_m[:], in0=m_bf[:], scalar1=-1.0, scalar2=1.0, op0=ALU.mult, op1=ALU.add
             )
+            nc.vector.tensor_scalar(out=half_m[:], in0=m_bf[:], scalar1=0.5, scalar2=None, op0=ALU.mult)
+            for t in range(TOKEN_TILES):
+                nc.vector.tensor_tensor(
+                    out=mi_bias[:, t, :], in0=mi_sb[:, t, :], in1=bias_all[:, GATES.index("F"), :], op=ALU.add
+                )
+
+        work = ctx.enter_context(tc.tile_pool(name="work", bufs=2))
 
         live = {}
 
-        def place(unit):
-            chunk, t = divmod(unit, TOKEN_TILES)
-            return t, slice(chunk * CHUNK, (chunk + 1) * CHUNK)
-
-        def gate_matmuls(unit):
+        def if_matmuls(unit):
             t, cols = place(unit)
             tokens = slice(t * P, (t + 1) * P)
-            for i, gate in enumerate(GATES):
-                acc = psum.tile([P, CHUNK], F32, tag="bank")
+            for gate in ("I", "F"):
+                acc = psum.tile([P, CHUNK], F32, tag="if", bufs=4)
                 for c in range(PASSES):
                     nc.tensor.matmul_mx(
                         out=acc[:],
                         lhsT=x_codes[:, c, tokens].bitcast(FP8X4),
                         lhsT_scale=x_scales[:, c, tokens],
                         rhs=codes[gate][:, c, cols].bitcast(FP8X4),
-                        rhs_scale=planes[4 * i : P, c, cols],
+                        rhs_scale=planes[gate][plane_offset[gate] : P, c, cols],
                         start=(c == 0),
                         stop=(c == PASSES - 1),
                     )
                 live[gate, unit] = acc
+
+        def flip_tanh_biases():
+            nc.vector.tensor_tensor(out=tanh_rows[:], in0=tanh_w_rows[:], in1=tanh_r_rows[:], op=ALU.add)
+            flipped = psum.tile([P, P], F32, tag="tanh_out")
+            nc.tensor.transpose(flipped[:], tanh_rows[:], ident[:])
+            nc.vector.tensor_copy(out=tanh_bias[:, 0, :], in_=flipped[:, 0:COLUMN_TILES])
+            nc.vector.tensor_scalar(
+                out=tanh_bias[:, 1, :], in0=flipped[:, COLUMN_TILES : 2 * COLUMN_TILES],
+                scalar1=0.5, scalar2=None, op0=ALU.mult,
+            )
+
+        def tanh_group(group):
+            chunk, rest = divmod(group, GROUPS_PER_CHUNK)
+            which, quarter = divmod(rest, CHUNK // P)
+            gate = TANH_GATES[which]
+            column_tile = chunk * (CHUNK // P) + quarter
+            cols = slice(column_tile * P, (column_tile + 1) * P)
+            acc = psum.tile([P, TOKENS], F32, tag="tanh_in")
+            for c in range(PASSES):
+                nc.tensor.matmul_mx(
+                    out=acc[:],
+                    lhsT=codes[gate][:, c, cols].bitcast(FP8X4),
+                    lhsT_scale=planes[gate][plane_offset[gate] : P, c, cols],
+                    rhs=x_codes[:, c, :].bitcast(FP8X4),
+                    rhs_scale=x_scales[:, c, :],
+                    start=(c == 0),
+                    stop=(c == PASSES - 1),
+                )
+            by_column = work.tile([P, TOKENS], F32, bufs=TANH_GROUPS)
+            nc.scalar.activation(
+                out=by_column[:], in_=acc[:], func=ACT.Tanh,
+                bias=tanh_bias[:, which, column_tile : column_tile + 1], scale=(1.0 if gate == "Z" else 0.5),
+            )
+            live[gate, "column tile", column_tile] = by_column
+
+        def back_transposes(unit):
+            chunk, t = divmod(unit, TOKEN_TILES)
+            for gate in TANH_GATES:
+                by_token_ps = psum.tile([P, CHUNK], F32, tag="tanh_out")
+                for quarter in range(CHUNK // P):
+                    nc.tensor.transpose(
+                        by_token_ps[:, quarter * P : (quarter + 1) * P],
+                        live[gate, "column tile", chunk * (CHUNK // P) + quarter][:, t * P : (t + 1) * P],
+                        ident[:],
+                    )
+                live[gate, unit] = by_token_ps
 
         def leave_psum(unit):
             t, cols = place(unit)
@@ -204,35 +283,29 @@ def tile_customlstmcell_kernel(
             f_pre = work.tile([P, CHUNK], F32, bufs=1)
             m_t = work.tile([P, CHUNK], F32, bufs=3)
             d = work.tile([P, CHUNK], F32)
-            z = work.tile([P, CHUNK], F32)
-            o = work.tile([P, CHUNK], F32)
             nc.vector.tensor_tensor(out=i_pre[:], in0=live["I", unit][:], in1=bias_all[:, GATES.index("I"), cols], op=ALU.add)
             nc.vector.tensor_tensor(out=f_pre[:], in0=live["F", unit][:], in1=mi_bias[:, t, cols], op=ALU.add)
             nc.vector.tensor_tensor(out=d[:], in0=f_pre[:], in1=i_pre[:], op=ALU.subtract)
             nc.vector.tensor_tensor(out=m_t[:], in0=f_pre[:], in1=i_pre[:], op=ALU.max)
             nc.sync.dma_start(out=m_out[:, t, cols], in_=m_t[:])
-            nc.vector.tensor_tensor(out=z[:], in0=live["Z", unit][:], in1=bias_all[:, GATES.index("Z"), cols], op=ALU.add)
-            nc.vector.tensor_tensor(out=o[:], in0=live["O", unit][:], in1=bias_all[:, GATES.index("O"), cols], op=ALU.add)
-            live["d", unit], live["z", unit], live["o", unit] = d, z, o
+            live["d", unit] = d
 
         def gate_functions(unit):
             t, cols = place(unit)
-            d, z, o = live["d", unit], live["z", unit], live["o", unit]
-            e_i = work.tile([P, CHUNK], F32)
-            g = work.tile([P, CHUNK], F32)
+            d = live["d", unit]
+            e_i = work.tile([P, CHUNK], F32, bufs=CELL_LAG + 1)
+            g = work.tile([P, CHUNK], F32, bufs=CELL_LAG + 1)
             nc.scalar.activation(out=e_i[:], in_=d[:], func=ACT.Exp, scale=-1.0)
             nc.scalar.activation(out=d[:], in_=d[:], func=ACT.Relu, scale=-1.0)
             nc.scalar.activation(out=d[:], in_=d[:], func=ACT.Exp, scale=-1.0)
             nc.scalar.activation(
                 out=g[:], in_=d[:], func=ACT.Identity, scale=m_f32[:, t : t + 1], bias=one_minus_m[:, t : t + 1]
             )
-            nc.scalar.activation(out=z[:], in_=z[:], func=ACT.Tanh)
-            nc.scalar.activation(out=o[:], in_=o[:], func=ACT.Tanh, scale=0.5)
             live["e_i", unit], live["g", unit] = e_i, g
 
         def normaliser(unit):
             t, cols = place(unit)
-            n_t = work.tile([P, CHUNK], F32, bufs=3)
+            n_t = work.tile([P, CHUNK], F32, bufs=LN_GROUP + RECIPROCAL_LAG - 1)
             nc.vector.tensor_tensor(out=n_t[:], in0=live["d", unit][:], in1=ni_sb[:, t, cols], op=ALU.mult)
             nc.vector.scalar_tensor_tensor(
                 out=n_t[:], in0=live["e_i", unit][:], scalar=1.0, in1=n_t[:], op0=ALU.min, op1=ALU.add
@@ -240,32 +313,32 @@ def tile_customlstmcell_kernel(
             nc.sync.dma_start(out=n_out[:, t, cols], in_=n_t[:])
             live["n_t", unit] = n_t
 
-        def cell(unit):
-            t, cols = place(unit)
-            z = live["z", unit]
-            kept = work.tile([P, CHUNK], F32, bufs=1)
-            c_t = work.tile([P, CHUNK], F32, bufs=3)
-            oc = work.tile([P, CHUNK], F32, bufs=3)
-            nc.vector.tensor_tensor(out=kept[:], in0=live["g", unit][:], in1=ci_sb[:, t, cols], op=ALU.mult)
-            nc.vector.scalar_tensor_tensor(
-                out=z[:], in0=live["e_i", unit][:], scalar=1.0, in1=z[:], op0=ALU.min, op1=ALU.mult
-            )
-            nc.vector.scalar_tensor_tensor(
-                out=c_t[:], in0=z[:], scalar=m_f32[:, t : t + 1], in1=kept[:], op0=ALU.mult, op1=ALU.add
-            )
-            nc.sync.dma_start(out=c_out[:, t, cols], in_=c_t[:])
-            nc.vector.scalar_tensor_tensor(
-                out=oc[:], in0=live["o", unit][:], scalar=1.0, in1=c_t[:], op0=ALU.add, op1=ALU.mult
-            )
-            live["oc", unit] = oc
-
         def reciprocals(units):
             for unit in units:
-                r = work.tile([P, CHUNK], F32, bufs=2 * LN_GROUP)
+                r = work.tile([P, CHUNK], F32, bufs=LN_GROUP)
                 nc.scalar.activation(out=r[:], in_=live["n_t", unit][:], func=ACT.Ln)
                 live["r", unit] = r
             for unit in units:
                 nc.scalar.activation(out=live["r", unit][:], in_=live["r", unit][:], func=ACT.Exp, scale=-1.0)
+
+        def cell(unit):
+            t, cols = place(unit)
+            kept = work.tile([P, CHUNK], F32, bufs=1)
+            fresh = work.tile([P, CHUNK], F32, bufs=1)
+            c_t = work.tile([P, CHUNK], F32, bufs=3)
+            oc = work.tile([P, CHUNK], F32, bufs=LN_GROUP)
+            nc.vector.tensor_tensor(out=kept[:], in0=live["g", unit][:], in1=ci_sb[:, t, cols], op=ALU.mult)
+            nc.vector.scalar_tensor_tensor(
+                out=fresh[:], in0=live["e_i", unit][:], scalar=1.0, in1=live["Z", unit][:], op0=ALU.min, op1=ALU.mult
+            )
+            nc.vector.scalar_tensor_tensor(
+                out=c_t[:], in0=fresh[:], scalar=m_f32[:, t : t + 1], in1=kept[:], op0=ALU.mult, op1=ALU.add
+            )
+            nc.sync.dma_start(out=c_out[:, t, cols], in_=c_t[:])
+            nc.vector.scalar_tensor_tensor(
+                out=oc[:], in0=live["O", unit][:], scalar=1.0, in1=c_t[:], op0=ALU.add, op1=ALU.mult
+            )
+            live["oc", unit] = oc
 
         def hidden(unit):
             t, cols = place(unit)
@@ -278,21 +351,31 @@ def tile_customlstmcell_kernel(
             )
             nc.sync.dma_start(out=h_out[:, t, cols], in_=r[:])
 
-        gate_matmuls(0)
-        gate_matmuls(1)
-        for step in range(UNITS + 2):
+        def ln_group_ending_at(unit):
+            if 0 <= unit < UNITS and unit % LN_GROUP == LN_GROUP - 1:
+                return range(unit - LN_GROUP + 1, unit + 1)
+            return range(0)
+
+        if_matmuls(0)
+        if_matmuls(1)
+        for step in range(UNITS + CELL_LAG):
             if step < UNITS:
                 leave_psum(step)
                 if step + 2 < UNITS:
-                    gate_matmuls(step + 2)
+                    if_matmuls(step + 2)
                 gate_functions(step)
-            done = step - 1
-            if 0 <= done < UNITS:
-                normaliser(done)
-                if done % LN_GROUP == LN_GROUP - 1:
-                    reciprocals(range(done - LN_GROUP + 1, done + 1))
-                cell(done)
-            ready = step - 2
-            if ready >= 0 and ready % LN_GROUP == LN_GROUP - 1:
-                for unit in range(ready - LN_GROUP + 1, ready + 1):
-                    hidden(unit)
+                if step < len(GATES):
+                    load_codes(GATES[step], 1)
+                if step == 0:
+                    flip_tanh_biases()
+                for group in range(step * TANH_GROUPS_PER_STEP, (step + 1) * TANH_GROUPS_PER_STEP):
+                    tanh_group(group)
+            if 0 <= step - 1 < UNITS:
+                normaliser(step - 1)
+            reciprocals(ln_group_ending_at(step - RECIPROCAL_LAG))
+            if 0 <= step - CELL_LAG:
+                cell(step - CELL_LAG)
+            if 0 <= step - CELL_LAG + 1 < UNITS:
+                back_transposes(step - CELL_LAG + 1)
+            for unit in ln_group_ending_at(step - CELL_LAG):
+                hidden(unit)

@@ -28,9 +28,11 @@ TANH_GATES = ("Z", "O")
 TANH_GROUPS = len(TANH_GATES) * COLUMN_TILES
 GROUPS_PER_CHUNK = TANH_GROUPS // CHUNKS
 TANH_GROUPS_PER_STEP = TANH_GROUPS // UNITS
-LN_GROUP = 4
+LN_GROUP = 2
 CELL_LAG = GROUPS_PER_CHUNK // TANH_GROUPS_PER_STEP
-RECIPROCAL_LAG = CELL_LAG - 1
+HIDDEN_LAG = CELL_LAG + 1
+RECIPROCAL_LAG = 2
+SMALLEST_NORMAL = 2.0 ** -126
 
 FLOPS = 2 * TOKENS * (DFF + D) * 4 * DFF
 
@@ -89,6 +91,7 @@ def tile_customlstmcell_kernel(
         tanh_r_rows = keep.tile([P, P], BF16)
         tanh_rows = keep.tile([P, P], F32)
         m_f32 = keep.tile([P, TOKEN_TILES], F32)
+        m_floor = keep.tile([P, TOKEN_TILES], F32)
         one_minus_m = keep.tile([P, TOKEN_TILES], F32)
         half_m = keep.tile([P, TOKEN_TILES], F32)
 
@@ -201,6 +204,7 @@ def tile_customlstmcell_kernel(
                     nc.scalar.copy(out=bias_all[:, i, cols], in_=spread[:])
 
             nc.vector.tensor_copy(out=m_f32[:], in_=m_bf[:])
+            nc.vector.tensor_scalar(out=m_floor[:], in0=m_bf[:], scalar1=SMALLEST_NORMAL, scalar2=None, op0=ALU.max)
             nc.vector.tensor_scalar(
                 out=one_minus_m[:], in0=m_bf[:], scalar1=-1.0, scalar2=1.0, op0=ALU.mult, op1=ALU.add
             )
@@ -214,7 +218,17 @@ def tile_customlstmcell_kernel(
 
         live = {}
 
+        def valid(unit):
+            return 0 <= unit < UNITS
+
+        def new_tile(name, unit, bufs):
+            made = work.tile([P, CHUNK], F32, tag=name, name=name, bufs=bufs)
+            live[name, unit] = made
+            return made
+
         def if_matmuls(unit):
+            if not valid(unit):
+                return
             t, cols = place(unit)
             tokens = slice(t * P, (t + 1) * P)
             for gate in ("I", "F"):
@@ -242,6 +256,8 @@ def tile_customlstmcell_kernel(
             )
 
         def tanh_group(group):
+            if not 0 <= group < TANH_GROUPS:
+                return
             chunk, rest = divmod(group, GROUPS_PER_CHUNK)
             which, quarter = divmod(rest, CHUNK // P)
             gate = TANH_GATES[which]
@@ -266,6 +282,8 @@ def tile_customlstmcell_kernel(
             live[gate, "column tile", column_tile] = by_column
 
         def back_transposes(unit):
+            if not valid(unit):
+                return
             chunk, t = divmod(unit, TOKEN_TILES)
             for gate in TANH_GATES:
                 by_token_ps = psum.tile([P, CHUNK], F32, tag="tanh_out")
@@ -277,105 +295,145 @@ def tile_customlstmcell_kernel(
                     )
                 live[gate, unit] = by_token_ps
 
-        def leave_psum(unit):
-            t, cols = place(unit)
-            i_pre = work.tile([P, CHUNK], F32, bufs=1)
-            f_pre = work.tile([P, CHUNK], F32, bufs=1)
-            m_t = work.tile([P, CHUNK], F32, bufs=3)
-            d = work.tile([P, CHUNK], F32)
-            nc.vector.tensor_tensor(out=i_pre[:], in0=live["I", unit][:], in1=bias_all[:, GATES.index("I"), cols], op=ALU.add)
-            nc.vector.tensor_tensor(out=f_pre[:], in0=live["F", unit][:], in1=mi_bias[:, t, cols], op=ALU.add)
-            nc.vector.tensor_tensor(out=d[:], in0=f_pre[:], in1=i_pre[:], op=ALU.subtract)
-            nc.vector.tensor_tensor(out=m_t[:], in0=f_pre[:], in1=i_pre[:], op=ALU.max)
-            nc.sync.dma_start(out=m_out[:, t, cols], in_=m_t[:])
-            live["d", unit] = d
+        def input_gate(unit):
+            if valid(unit):
+                t, cols = place(unit)
+                nc.vector.tensor_tensor(
+                    out=new_tile("i_pre", unit, 1)[:], in0=live["I", unit][:],
+                    in1=bias_all[:, GATES.index("I"), cols], op=ALU.add,
+                )
 
-        def gate_functions(unit):
-            t, cols = place(unit)
-            d = live["d", unit]
-            e_i = work.tile([P, CHUNK], F32, bufs=CELL_LAG + 1)
-            g = work.tile([P, CHUNK], F32, bufs=CELL_LAG + 1)
-            nc.scalar.activation(out=e_i[:], in_=d[:], func=ACT.Exp, scale=-1.0)
-            nc.scalar.activation(out=d[:], in_=d[:], func=ACT.Relu, scale=-1.0)
-            nc.scalar.activation(out=d[:], in_=d[:], func=ACT.Exp, scale=-1.0)
-            nc.scalar.activation(
-                out=g[:], in_=d[:], func=ACT.Identity, scale=m_f32[:, t : t + 1], bias=one_minus_m[:, t : t + 1]
-            )
-            live["e_i", unit], live["g", unit] = e_i, g
+        def forget_gate(unit):
+            if valid(unit):
+                t, cols = place(unit)
+                nc.vector.tensor_tensor(
+                    out=new_tile("f_pre", unit, 1)[:], in0=live["F", unit][:], in1=mi_bias[:, t, cols], op=ALU.add
+                )
+
+        def difference(unit):
+            if valid(unit):
+                nc.vector.tensor_tensor(
+                    out=new_tile("d", unit, 2)[:], in0=live["f_pre", unit][:], in1=live["i_pre", unit][:], op=ALU.subtract
+                )
+
+        def stabiliser(unit):
+            if valid(unit):
+                t, cols = place(unit)
+                m_t = new_tile("m_t", unit, 3)
+                nc.vector.tensor_tensor(out=m_t[:], in0=live["f_pre", unit][:], in1=live["i_pre", unit][:], op=ALU.max)
+                nc.sync.dma_start(out=m_out[:, t, cols], in_=m_t[:])
+
+        def exponentials(unit):
+            if valid(unit):
+                d = live["d", unit]
+                nc.scalar.activation(out=new_tile("e_i", unit, CELL_LAG + 1)[:], in_=d[:], func=ACT.Exp, scale=-1.0)
+                nc.scalar.activation(out=d[:], in_=d[:], func=ACT.Exp)
+
+        def blend_factor(unit):
+            if valid(unit):
+                t, cols = place(unit)
+                nc.scalar.activation(
+                    out=new_tile("g", unit, CELL_LAG + 1)[:], in_=live["d", unit][:], func=ACT.Identity,
+                    scale=m_floor[:, t : t + 1], bias=one_minus_m[:, t : t + 1],
+                )
+
+        def forgotten_n(unit):
+            if valid(unit):
+                t, cols = place(unit)
+                nc.vector.scalar_tensor_tensor(
+                    out=new_tile("n_t", unit, LN_GROUP + RECIPROCAL_LAG)[:], in0=live["d", unit][:], scalar=1.0,
+                    in1=ni_sb[:, t, cols], op0=ALU.min, op1=ALU.mult,
+                )
 
         def normaliser(unit):
-            t, cols = place(unit)
-            n_t = work.tile([P, CHUNK], F32, bufs=LN_GROUP + RECIPROCAL_LAG - 1)
-            nc.vector.tensor_tensor(out=n_t[:], in0=live["d", unit][:], in1=ni_sb[:, t, cols], op=ALU.mult)
-            nc.vector.scalar_tensor_tensor(
-                out=n_t[:], in0=live["e_i", unit][:], scalar=1.0, in1=n_t[:], op0=ALU.min, op1=ALU.add
-            )
-            nc.sync.dma_start(out=n_out[:, t, cols], in_=n_t[:])
-            live["n_t", unit] = n_t
+            if valid(unit):
+                t, cols = place(unit)
+                n_t = live["n_t", unit]
+                nc.vector.scalar_tensor_tensor(
+                    out=n_t[:], in0=live["e_i", unit][:], scalar=1.0, in1=n_t[:], op0=ALU.min, op1=ALU.add
+                )
+                nc.sync.dma_start(out=n_out[:, t, cols], in_=n_t[:])
 
-        def reciprocals(units):
-            for unit in units:
-                r = work.tile([P, CHUNK], F32, bufs=LN_GROUP)
-                nc.scalar.activation(out=r[:], in_=live["n_t", unit][:], func=ACT.Ln)
-                live["r", unit] = r
-            for unit in units:
-                nc.scalar.activation(out=live["r", unit][:], in_=live["r", unit][:], func=ACT.Exp, scale=-1.0)
+        def reciprocals(last):
+            if valid(last) and last % LN_GROUP == LN_GROUP - 1:
+                units = range(last - LN_GROUP + 1, last + 1)
+                for unit in units:
+                    nc.scalar.activation(out=new_tile("r", unit, 2 * LN_GROUP)[:], in_=live["n_t", unit][:], func=ACT.Ln)
+                for unit in units:
+                    nc.scalar.activation(out=live["r", unit][:], in_=live["r", unit][:], func=ACT.Exp, scale=-1.0)
+
+        def kept_cell(unit):
+            if valid(unit):
+                t, cols = place(unit)
+                nc.vector.scalar_tensor_tensor(
+                    out=new_tile("kept", unit, 1)[:], in0=live["g", unit][:], scalar=1.0, in1=ci_sb[:, t, cols],
+                    op0=ALU.min, op1=ALU.mult,
+                )
+
+        def fresh_cell(unit):
+            if valid(unit):
+                nc.vector.scalar_tensor_tensor(
+                    out=new_tile("fresh", unit, 1)[:], in0=live["e_i", unit][:], scalar=1.0, in1=live["Z", unit][:],
+                    op0=ALU.min, op1=ALU.mult,
+                )
 
         def cell(unit):
-            t, cols = place(unit)
-            kept = work.tile([P, CHUNK], F32, bufs=1)
-            fresh = work.tile([P, CHUNK], F32, bufs=1)
-            c_t = work.tile([P, CHUNK], F32, bufs=3)
-            oc = work.tile([P, CHUNK], F32, bufs=LN_GROUP)
-            nc.vector.tensor_tensor(out=kept[:], in0=live["g", unit][:], in1=ci_sb[:, t, cols], op=ALU.mult)
-            nc.vector.scalar_tensor_tensor(
-                out=fresh[:], in0=live["e_i", unit][:], scalar=1.0, in1=live["Z", unit][:], op0=ALU.min, op1=ALU.mult
-            )
-            nc.vector.scalar_tensor_tensor(
-                out=c_t[:], in0=fresh[:], scalar=m_f32[:, t : t + 1], in1=kept[:], op0=ALU.mult, op1=ALU.add
-            )
-            nc.sync.dma_start(out=c_out[:, t, cols], in_=c_t[:])
-            nc.vector.scalar_tensor_tensor(
-                out=oc[:], in0=live["O", unit][:], scalar=1.0, in1=c_t[:], op0=ALU.add, op1=ALU.mult
-            )
-            live["oc", unit] = oc
+            if valid(unit):
+                t, cols = place(unit)
+                c_t = new_tile("c_t", unit, 3)
+                nc.vector.scalar_tensor_tensor(
+                    out=c_t[:], in0=live["fresh", unit][:], scalar=m_f32[:, t : t + 1], in1=live["kept", unit][:],
+                    op0=ALU.mult, op1=ALU.add,
+                )
+                nc.sync.dma_start(out=c_out[:, t, cols], in_=c_t[:])
+
+        def gated_cell(unit):
+            if valid(unit):
+                nc.vector.scalar_tensor_tensor(
+                    out=new_tile("oc", unit, 2)[:], in0=live["O", unit][:], scalar=1.0, in1=live["c_t", unit][:],
+                    op0=ALU.add, op1=ALU.mult,
+                )
+
+        def normalised_cell(unit):
+            if valid(unit):
+                t, cols = place(unit)
+                r = live["r", unit]
+                nc.vector.scalar_tensor_tensor(
+                    out=r[:], in0=live["oc", unit][:], scalar=half_m[:, t : t + 1], in1=r[:], op0=ALU.mult, op1=ALU.mult
+                )
 
         def hidden(unit):
-            t, cols = place(unit)
-            r = live["r", unit]
-            nc.vector.scalar_tensor_tensor(
-                out=r[:], in0=live["oc", unit][:], scalar=half_m[:, t : t + 1], in1=r[:], op0=ALU.mult, op1=ALU.mult
-            )
-            nc.vector.scalar_tensor_tensor(
-                out=r[:], in0=hi_sb[:, t, cols], scalar=one_minus_m[:, t : t + 1], in1=r[:], op0=ALU.mult, op1=ALU.add
-            )
-            nc.sync.dma_start(out=h_out[:, t, cols], in_=r[:])
-
-        def ln_group_ending_at(unit):
-            if 0 <= unit < UNITS and unit % LN_GROUP == LN_GROUP - 1:
-                return range(unit - LN_GROUP + 1, unit + 1)
-            return range(0)
+            if valid(unit):
+                t, cols = place(unit)
+                r = live["r", unit]
+                nc.vector.scalar_tensor_tensor(
+                    out=r[:], in0=hi_sb[:, t, cols], scalar=one_minus_m[:, t : t + 1], in1=r[:], op0=ALU.mult, op1=ALU.add
+                )
+                nc.sync.dma_start(out=h_out[:, t, cols], in_=r[:])
 
         if_matmuls(0)
         if_matmuls(1)
-        for step in range(UNITS + CELL_LAG):
-            if step < UNITS:
-                leave_psum(step)
-                if step + 2 < UNITS:
-                    if_matmuls(step + 2)
-                gate_functions(step)
-                if step < len(GATES):
-                    load_codes(GATES[step], 1)
-                if step == 0:
-                    flip_tanh_biases()
-                for group in range(step * TANH_GROUPS_PER_STEP, (step + 1) * TANH_GROUPS_PER_STEP):
-                    tanh_group(group)
-            if 0 <= step - 1 < UNITS:
-                normaliser(step - 1)
-            reciprocals(ln_group_ending_at(step - RECIPROCAL_LAG))
-            if 0 <= step - CELL_LAG:
-                cell(step - CELL_LAG)
-            if 0 <= step - CELL_LAG + 1 < UNITS:
-                back_transposes(step - CELL_LAG + 1)
-            for unit in ln_group_ending_at(step - CELL_LAG):
-                hidden(unit)
+        for step in range(UNITS + HIDDEN_LAG):
+            input_gate(step)
+            forget_gate(step)
+            forgotten_n(step - 1)
+            difference(step)
+            normaliser(step - 1)
+            stabiliser(step)
+            if_matmuls(step + 2)
+            if step < len(GATES):
+                load_codes(GATES[step], 1)
+            if step == 0:
+                flip_tanh_biases()
+            exponentials(step)
+            tanh_group(TANH_GROUPS_PER_STEP * step)
+            blend_factor(step)
+            tanh_group(TANH_GROUPS_PER_STEP * step + 1)
+            reciprocals(step - RECIPROCAL_LAG)
+            kept_cell(step - CELL_LAG)
+            fresh_cell(step - CELL_LAG)
+            normalised_cell(step - HIDDEN_LAG)
+            cell(step - CELL_LAG)
+            hidden(step - HIDDEN_LAG)
+            gated_cell(step - CELL_LAG)
+            back_transposes(step - CELL_LAG + 1)

@@ -29,9 +29,10 @@ TANH_GROUPS = len(TANH_GATES) * COLUMN_TILES
 GROUPS_PER_CHUNK = TANH_GROUPS // CHUNKS
 TANH_GROUPS_PER_STEP = TANH_GROUPS // UNITS
 LN_GROUP = 2
-CELL_LAG = GROUPS_PER_CHUNK // TANH_GROUPS_PER_STEP
+TANH_FIRST_STEP = 3
+CELL_LAG = TANH_FIRST_STEP + GROUPS_PER_CHUNK // TANH_GROUPS_PER_STEP
 HIDDEN_LAG = CELL_LAG + 1
-RECIPROCAL_LAG = 2
+RECIPROCAL_LAG = HIDDEN_LAG - 3
 SMALLEST_NORMAL = 2.0 ** -126
 
 FLOPS = 2 * TOKENS * (DFF + D) * 4 * DFF
@@ -64,8 +65,6 @@ def tile_customlstmcell_kernel(
         ctx.enter_context(tc.manual_schedule())
 
         hi_sb = keep.tile([P, TOKEN_TILES, DFF], BF16)
-        zi_sb = keep.tile([P, TOKEN_TILES, D], BF16)
-        mi_sb = keep.tile([P, TOKEN_TILES, DFF], BF16)
         ni_sb = keep.tile([P, TOKEN_TILES, DFF], BF16)
         ci_sb = keep.tile([P, TOKEN_TILES, DFF], BF16)
         m_bf = keep.tile([P, TOKEN_TILES], BF16)
@@ -111,6 +110,8 @@ def tile_customlstmcell_kernel(
             )
 
         with tc.tile_pool(name="prep", bufs=1) as prep:
+            zi_sb = prep.tile([P, TOKEN_TILES, D], BF16)
+            mi_sb = prep.tile([P, TOKEN_TILES, DFF], BF16)
             bias_rows = prep.tile([P, 2, DFF], BF16)
             grouped = []
             for c in range(PASSES):
@@ -152,6 +153,8 @@ def tile_customlstmcell_kernel(
             for gate in ("I", "F"):
                 load_codes(gate, 0)
             nc.sync.dma_start(out=ni_sb[:], in_=by_token(Ni))
+            for gate in ("I", "F"):
+                load_codes(gate, 1)
             for i, gate in enumerate(TANH_GATES):
                 rows = slice(i * COLUMN_TILES, (i + 1) * COLUMN_TILES)
                 nc.sync.dma_start(out=tanh_w_rows[rows, :], in_=w_bias[gate].rearrange("(i n) -> i n", n=P))
@@ -161,6 +164,8 @@ def tile_customlstmcell_kernel(
             for gate in TANH_GATES:
                 load_codes(gate, 0)
             nc.sync.dma_start(out=ci_sb[:], in_=by_token(Ci))
+            for gate in TANH_GATES:
+                load_codes(gate, 1)
 
             x_blocks = ((hi_sb, 0), (hi_sb, 1), (zi_sb, 0))
 
@@ -321,7 +326,7 @@ def tile_customlstmcell_kernel(
                 t, cols = place(unit)
                 m_t = new_tile("m_t", unit, 3)
                 nc.vector.tensor_tensor(out=m_t[:], in0=live["f_pre", unit][:], in1=live["i_pre", unit][:], op=ALU.max)
-                nc.sync.dma_start(out=m_out[:, t, cols], in_=m_t[:])
+                nc.gpsimd.dma_start(out=m_out[:, t, cols], in_=m_t[:])
 
         def exponentials(unit):
             if valid(unit):
@@ -352,7 +357,7 @@ def tile_customlstmcell_kernel(
                 nc.vector.scalar_tensor_tensor(
                     out=n_t[:], in0=live["e_i", unit][:], scalar=1.0, in1=n_t[:], op0=ALU.min, op1=ALU.add
                 )
-                nc.sync.dma_start(out=n_out[:, t, cols], in_=n_t[:])
+                nc.gpsimd.dma_start(out=n_out[:, t, cols], in_=n_t[:])
 
         def reciprocals(last):
             if valid(last) and last % LN_GROUP == LN_GROUP - 1:
@@ -421,14 +426,12 @@ def tile_customlstmcell_kernel(
             normaliser(step - 1)
             stabiliser(step)
             if_matmuls(step + 2)
-            if step < len(GATES):
-                load_codes(GATES[step], 1)
-            if step == 0:
+            if step == TANH_FIRST_STEP:
                 flip_tanh_biases()
             exponentials(step)
-            tanh_group(TANH_GROUPS_PER_STEP * step)
+            tanh_group(TANH_GROUPS_PER_STEP * (step - TANH_FIRST_STEP))
             blend_factor(step)
-            tanh_group(TANH_GROUPS_PER_STEP * step + 1)
+            tanh_group(TANH_GROUPS_PER_STEP * (step - TANH_FIRST_STEP) + 1)
             reciprocals(step - RECIPROCAL_LAG)
             kept_cell(step - CELL_LAG)
             fresh_cell(step - CELL_LAG)

@@ -15,6 +15,7 @@ ACT = mybir.ActivationFunctionType
 P = 128
 TOKENS = 512
 TOKEN_TILES = TOKENS // P
+HALF = TOKENS // 2
 D = 512
 DFF = 1024
 K_PASS = 512
@@ -23,16 +24,9 @@ CHUNK = 512
 CHUNKS = DFF // CHUNK
 UNITS = CHUNKS * TOKEN_TILES
 COLUMN_TILES = DFF // P
+TILES_PER_CHUNK = CHUNK // P
 GATES = ("I", "F", "Z", "O")
-TANH_GATES = ("Z", "O")
-TANH_GROUPS = len(TANH_GATES) * COLUMN_TILES
-GROUPS_PER_CHUNK = TANH_GROUPS // CHUNKS
-TANH_GROUPS_PER_STEP = TANH_GROUPS // UNITS
-LN_GROUP = 2
-TANH_FIRST_STEP = 3
-CELL_LAG = TANH_FIRST_STEP + GROUPS_PER_CHUNK // TANH_GROUPS_PER_STEP
-HIDDEN_LAG = CELL_LAG + 1
-RECIPROCAL_LAG = HIDDEN_LAG - 3
+FLIPPED = ("I", "Z", "O")
 SMALLEST_NORMAL = 2.0 ** -126
 
 FLOPS = 2 * TOKENS * (DFF + D) * 4 * DFF
@@ -61,38 +55,61 @@ def tile_customlstmcell_kernel(
 
     with ExitStack() as ctx:
         keep = ctx.enter_context(tc.tile_pool(name="keep", bufs=1))
+        columns = ctx.enter_context(tc.tile_pool(name="columns", bufs=2 * COLUMN_TILES))
+        rotate = ctx.enter_context(tc.tile_pool(name="rotate", bufs=3))
         psum = ctx.enter_context(tc.psum_pool(name="psum", bufs=2))
         ctx.enter_context(tc.manual_schedule())
 
         hi_sb = keep.tile([P, TOKEN_TILES, DFF], BF16)
+        zi_sb = keep.tile([P, TOKEN_TILES, D], BF16)
+        mi_sb = keep.tile([P, TOKEN_TILES, DFF], BF16)
         ni_sb = keep.tile([P, TOKEN_TILES, DFF], BF16)
         ci_sb = keep.tile([P, TOKEN_TILES, DFF], BF16)
-        m_bf = keep.tile([P, TOKEN_TILES], BF16)
         codes = {}
+        planes = {}
         for gate in GATES:
             gate_codes = keep.tile([P, PASSES, DFF], U32, align_bytes=64, name="codes_" + gate)
             codes[gate] = gate_codes
-        planes = {}
-        plane_offset = {}
-        for mates in (("I", "F"), TANH_GATES):
-            shared = keep.tile([P, PASSES, DFF], U8, align_bytes=64, name="planes_" + mates[0] + mates[1])
-            for k, gate in enumerate(mates):
-                planes[gate] = shared
-                plane_offset[gate] = 4 * k
+            gate_planes = keep.tile([P, DFF], U8, align_bytes=64, name="planes_" + gate)
+            planes[gate] = gate_planes
         x_codes = keep.tile([P, PASSES, TOKENS], U32, align_bytes=64)
         x_scales = keep.tile([P, PASSES, TOKENS], U8, align_bytes=64)
         ident = keep.tile([P, P], F32)
+        ident_bf = keep.tile([P, P], BF16)
         ones = keep.tile([P, P], BF16)
-        bias_all = keep.tile([P, 2, DFF], F32)
-        tanh_bias = keep.tile([P, len(TANH_GATES), COLUMN_TILES], F32)
-        mi_bias = keep.tile([P, TOKEN_TILES, DFF], F32)
-        tanh_w_rows = keep.tile([P, P], BF16)
-        tanh_r_rows = keep.tile([P, P], BF16)
-        tanh_rows = keep.tile([P, P], F32)
+        bias_rows = keep.tile([P, DFF], BF16)
+        w_rows, r_rows, sum_rows = {}, {}, {}
+        for name in ("I", "ZO"):
+            w_tile = keep.tile([P, P], BF16, name="w_rows_" + name)
+            r_tile = keep.tile([P, P], BF16, name="r_rows_" + name)
+            sum_tile = keep.tile([P, P], F32, name="sum_rows_" + name)
+            w_rows[name], r_rows[name], sum_rows[name] = w_tile, r_tile, sum_tile
+        column_bias = keep.tile([P, len(FLIPPED), COLUMN_TILES], F32)
+        m_bf = keep.tile([P, TOKEN_TILES], BF16)
         m_f32 = keep.tile([P, TOKEN_TILES], F32)
         m_floor = keep.tile([P, TOKEN_TILES], F32)
         one_minus_m = keep.tile([P, TOKEN_TILES], F32)
-        half_m = keep.tile([P, TOKEN_TILES], F32)
+        f_pre = keep.tile([P, UNITS, CHUNK], F32)
+        e_i = keep.tile([P, UNITS, CHUNK], F32)
+        g = keep.tile([P, UNITS, CHUNK], F32)
+        n_t = keep.tile([P, UNITS, CHUNK], F32)
+        grouped = []
+        for k in range(2 * PASSES):
+            grouped_k = keep.tile([P, HALF * 4], BF16, align_bytes=64, name="grouped%d" % k)
+            grouped.append(grouped_k)
+
+        make_identity(nc, ident[:])
+        for gate in ("I", "F"):
+            nc.vector.memset(planes[gate][:].bitcast(I32), 0)
+        nc.vector.memset(w_rows["I"][:], 0.0)
+        nc.vector.memset(r_rows["I"][:], 0.0)
+        nc.vector.memset(bias_rows[:].bitcast(I32), 0)
+        for gate in ("Z", "O"):
+            nc.vector.memset(planes[gate][:].bitcast(I32), 0)
+        nc.vector.memset(w_rows["ZO"][:], 0.0)
+        nc.vector.memset(r_rows["ZO"][:], 0.0)
+        nc.vector.memset(ones[:], 1.0)
+        nc.vector.tensor_copy(out=ident_bf[:], in_=ident[:])
 
         def place(unit):
             chunk, t = divmod(unit, TOKEN_TILES)
@@ -109,236 +126,212 @@ def tile_customlstmcell_kernel(
                 in_=r_words[gate].rearrange("g p n t -> p g (n t)").bitcast(I32)[:, :, cols],
             )
 
-        with tc.tile_pool(name="prep", bufs=1) as prep:
-            zi_sb = prep.tile([P, TOKEN_TILES, D], BF16)
-            mi_sb = prep.tile([P, TOKEN_TILES, DFF], BF16)
-            bias_rows = prep.tile([P, 2, DFF], BF16)
-            grouped = []
-            for c in range(PASSES):
-                grouped_c = prep.tile([P, TOKENS * 4], BF16, align_bytes=64, name="grouped%d" % c)
-                grouped.append(grouped_c)
+        def load_scales(gate, quadrants=(0, 1, 2, 3)):
+            for q in quadrants:
+                rows = slice(4 * q, 4 * q + 4)
+                nc.sync.dma_start(
+                    out=planes[gate][32 * q : 32 * q + 8, :].bitcast(I32),
+                    in_=w_scales[gate][:, rows, :].bitcast(I32),
+                )
+                nc.sync.dma_start(
+                    out=planes[gate][32 * q + 8 : 32 * q + 12, :].bitcast(I32),
+                    in_=r_scales[gate][0, rows, :].bitcast(I32),
+                )
 
-            nc.vector.memset(planes["I"][:].bitcast(I32), 0)
-            nc.vector.memset(planes["Z"][:].bitcast(I32), 0)
-            nc.vector.memset(bias_rows[:], 0.0)
-            nc.vector.memset(ones[:], 1.0)
-            nc.vector.memset(tanh_w_rows[:], 0.0)
-            nc.vector.memset(tanh_r_rows[:], 0.0)
-            make_identity(nc, ident[:])
-
-            def load_scales(gate):
-                for quadrant in range(4):
-                    rows = slice(4 * quadrant, 4 * quadrant + 4)
-                    first = 32 * quadrant + plane_offset[gate]
-                    nc.sync.dma_start(
-                        out=planes[gate][first : first + 4, 0:2, :].bitcast(I32),
-                        in_=w_scales[gate][:, rows, :].rearrange("g r n -> r g n").bitcast(I32),
-                    )
-                    nc.sync.dma_start(
-                        out=planes[gate][first : first + 4, 2:3, :].bitcast(I32),
-                        in_=r_scales[gate][:, rows, :].rearrange("g r n -> r g n").bitcast(I32),
-                    )
-
-            nc.scalar.dma_start(out=hi_sb[:], in_=by_token(Hi))
-            nc.scalar.dma_start(out=zi_sb[:], in_=by_token(Zi))
-            nc.sync.dma_start(
-                out=m_bf[:], in_=m.flatten_outer_dims().rearrange("(p t) o -> p (t o)", t=TOKEN_TILES)
-            )
-            for gate in ("F", "I"):
-                nc.sync.dma_start(out=bias_rows[0:1, GATES.index(gate), :], in_=w_bias[gate].unsqueeze(0))
-                nc.sync.dma_start(out=bias_rows[1:2, GATES.index(gate), :], in_=r_bias[gate].unsqueeze(0))
-            nc.sync.dma_start(out=mi_sb[:], in_=by_token(Mi))
-            for gate in ("I", "F"):
-                load_scales(gate)
-            for gate in ("I", "F"):
-                load_codes(gate, 0)
-            nc.sync.dma_start(out=ni_sb[:], in_=by_token(Ni))
-            for gate in ("I", "F"):
-                load_codes(gate, 1)
-            for i, gate in enumerate(TANH_GATES):
+        def load_column_biases(queue, name):
+            for i, gate in enumerate(name):
                 rows = slice(i * COLUMN_TILES, (i + 1) * COLUMN_TILES)
-                nc.sync.dma_start(out=tanh_w_rows[rows, :], in_=w_bias[gate].rearrange("(i n) -> i n", n=P))
-                nc.sync.dma_start(out=tanh_r_rows[rows, :], in_=r_bias[gate].rearrange("(i n) -> i n", n=P))
-            for gate in TANH_GATES:
-                load_scales(gate)
-            for gate in TANH_GATES:
-                load_codes(gate, 0)
-            nc.sync.dma_start(out=ci_sb[:], in_=by_token(Ci))
-            for gate in TANH_GATES:
-                load_codes(gate, 1)
+                queue.dma_start(out=w_rows[name][rows, :], in_=w_bias[gate].rearrange("(i n) -> i n", n=P))
+                queue.dma_start(out=r_rows[name][rows, :], in_=r_bias[gate].rearrange("(i n) -> i n", n=P))
 
-            x_blocks = ((hi_sb, 0), (hi_sb, 1), (zi_sb, 0))
+        load_scales("I", (0, 1, 2))
+        for half in range(2):
+            tiles = slice(2 * half, 2 * half + 2)
+            nc.sync.dma_start(out=hi_sb[:, tiles, :], in_=by_token(Hi)[:, tiles, :])
+            nc.sync.dma_start(out=zi_sb[:, tiles, :], in_=by_token(Zi)[:, tiles, :])
+        load_scales("I", (3,))
+        load_scales("F", (0, 1))
+        load_codes("I", 0)
+        load_scales("F", (2, 3))
+        load_codes("F", 0)
+        nc.sync.dma_start(out=mi_sb[:, :, 0:CHUNK], in_=by_token(Mi)[:, :, 0:CHUNK])
+        load_column_biases(nc.gpsimd, "I")
+        nc.gpsimd.dma_start(out=bias_rows[0:1, :], in_=w_bias["F"].unsqueeze(0))
+        nc.gpsimd.dma_start(out=bias_rows[1:2, :], in_=r_bias["F"].unsqueeze(0))
+        nc.gpsimd.dma_start(
+            out=m_bf[:], in_=m.flatten_outer_dims().rearrange("(p t) o -> p (t o)", t=TOKEN_TILES)
+        )
+        load_column_biases(nc.gpsimd, "ZO")
+        nc.sync.dma_start(out=ni_sb[:], in_=by_token(Ni))
+        load_codes("I", 1)
+        nc.sync.dma_start(out=mi_sb[:, :, CHUNK:DFF], in_=by_token(Mi)[:, :, CHUNK:DFF])
+        load_codes("F", 1)
+        load_scales("Z")
+        load_codes("Z", 0)
+        load_codes("Z", 1)
+        nc.sync.dma_start(out=ci_sb[:], in_=by_token(Ci))
+        load_scales("O")
+        load_codes("O", 0)
+        load_codes("O", 1)
 
-            def transpose_block(c):
-                x_sb, g = x_blocks[c]
-                x_words = x_sb[:].bitcast(F32)
-                out_words = grouped[c][:].bitcast(F32).rearrange("p (r u) -> p r u", u=2)
-                for half in range(2):
-                    xt = psum.tile([P, 2, 2 * P], F32, tag="if", bufs=4)
-                    for u in range(2):
-                        for s in range(2):
-                            nc.tensor.transpose(
-                                xt[:, u, s * P : (s + 1) * P],
-                                x_words[:, 2 * half + s, 256 * g + u : 256 * (g + 1) : 2],
-                                ident[:],
-                            )
-                    tokens = slice(half * 2 * P, (half + 1) * 2 * P)
-                    if half == 0:
-                        nc.vector.tensor_copy(out=out_words[:, tokens, :], in_=xt[:].rearrange("p u r -> p r u"))
-                    else:
-                        nc.scalar.copy(out=out_words[:, tokens, :], in_=xt[:].rearrange("p u r -> p r u"))
+        x_blocks = ((hi_sb, 0), (hi_sb, 1), (zi_sb, 0))
 
-            def quantise_block(c):
-                nc.vector.quantize_mx(
-                    out=x_codes[:, c, :].bitcast(FP8X4), scales=x_scales[:, c, :], in_=grouped[c][:]
-                )
+        def transpose_piece(half, c):
+            x_sb, group = x_blocks[c]
+            piece = half * PASSES + c
+            x_words = x_sb[:].bitcast(F32)
+            out_words = grouped[piece][:].bitcast(F32).rearrange("p (r u) -> p r u", u=2)
+            xt = psum.tile([P, 2, 2 * P], F32, tag=("back" if piece % 3 else "f"), bufs=(4 if piece % 3 else 2))
+            for u in range(2):
+                for s in range(2):
+                    nc.tensor.transpose(
+                        xt[:, u, s * P : (s + 1) * P],
+                        x_words[:, 2 * half + s, 256 * group + u : 256 * (group + 1) : 2],
+                        ident[:],
+                    )
+            copy = nc.vector.tensor_copy if piece % 2 == 0 else nc.scalar.copy
+            copy(out=out_words, in_=xt[:].rearrange("p u r -> p r u"))
 
-            transpose_block(0)
-            transpose_block(1)
-            quantise_block(0)
-            transpose_block(2)
-            quantise_block(1)
-            quantise_block(2)
-
-            for chunk in range(CHUNKS):
-                cols = slice(chunk * CHUNK, (chunk + 1) * CHUNK)
-                for gate in ("F", "I"):
-                    i = GATES.index(gate)
-                    spread = psum.tile([P, CHUNK], F32, tag="tanh_in")
-                    nc.tensor.matmul(out=spread[:], lhsT=ones[:], rhs=bias_rows[:, i, cols], start=True, stop=True)
-                    nc.scalar.copy(out=bias_all[:, i, cols], in_=spread[:])
-
-            nc.vector.tensor_copy(out=m_f32[:], in_=m_bf[:])
-            nc.vector.tensor_scalar(out=m_floor[:], in0=m_bf[:], scalar1=SMALLEST_NORMAL, scalar2=None, op0=ALU.max)
-            nc.vector.tensor_scalar(
-                out=one_minus_m[:], in0=m_bf[:], scalar1=-1.0, scalar2=1.0, op0=ALU.mult, op1=ALU.add
+        def quantise_piece(half, c):
+            tokens = slice(half * HALF, (half + 1) * HALF)
+            nc.vector.quantize_mx(
+                out=x_codes[:, c, tokens].bitcast(FP8X4), scales=x_scales[:, c, tokens],
+                in_=grouped[half * PASSES + c][:],
             )
-            nc.vector.tensor_scalar(out=half_m[:], in0=m_bf[:], scalar1=0.5, scalar2=None, op0=ALU.mult)
-            for t in range(TOKEN_TILES):
-                nc.vector.tensor_tensor(
-                    out=mi_bias[:, t, :], in0=mi_sb[:, t, :], in1=bias_all[:, GATES.index("F"), :], op=ALU.add
+
+        def flip_biases(name):
+            nc.vector.tensor_tensor(out=sum_rows[name][:], in0=w_rows[name][:], in1=r_rows[name][:], op=ALU.add)
+            flipped = psum.tile([P, P], F32, tag="back", bufs=4)
+            nc.tensor.transpose(flipped[:], sum_rows[name][:], ident[:])
+            return flipped
+
+        def finish_biases(name, flipped):
+            for i, gate in enumerate(name):
+                nc.vector.tensor_scalar(
+                    out=column_bias[:, FLIPPED.index(gate), :],
+                    in0=flipped[:, i * COLUMN_TILES : (i + 1) * COLUMN_TILES],
+                    scalar1=(-1.0 if gate == "O" else 1.0), scalar2=None, op0=ALU.mult,
                 )
 
-        work = ctx.enter_context(tc.tile_pool(name="work", bufs=2))
+        transpose_piece(0, 0)
+        transpose_piece(0, 1)
+        transpose_piece(0, 2)
+        quantise_piece(0, 0)
+        quantise_piece(0, 1)
+        quantise_piece(0, 2)
+        flipped_i = flip_biases("I")
+        transpose_piece(1, 0)
+        transpose_piece(1, 1)
+        finish_biases("I", flipped_i)
+        quantise_piece(1, 0)
+        transpose_piece(1, 2)
+        quantise_piece(1, 1)
+        quantise_piece(1, 2)
 
+        column_tiles = {}
         live = {}
 
         def valid(unit):
             return 0 <= unit < UNITS
 
-        def new_tile(name, unit, bufs):
-            made = work.tile([P, CHUNK], F32, tag=name, name=name, bufs=bufs)
-            live[name, unit] = made
-            return made
+        def prepare_m():
+            nc.vector.tensor_copy(out=m_f32[:], in_=m_bf[:])
+            nc.vector.tensor_scalar(out=m_floor[:], in0=m_bf[:], scalar1=SMALLEST_NORMAL, scalar2=None, op0=ALU.max)
+            nc.vector.tensor_scalar(
+                out=one_minus_m[:], in0=m_bf[:], scalar1=-1.0, scalar2=1.0, op0=ALU.mult, op1=ALU.add
+            )
 
-        def if_matmuls(unit):
+        def column_group(gate, column_tile, tokens=slice(0, TOKENS)):
+            cols = slice(column_tile * P, (column_tile + 1) * P)
+            acc = psum.tile([P, TOKENS], F32, tag="group")
+            for c in range(PASSES):
+                nc.tensor.matmul_mx(
+                    out=acc[:, tokens],
+                    lhsT=codes[gate][:, c, cols].bitcast(FP8X4),
+                    lhsT_scale=planes[gate][4 * c : P, cols],
+                    rhs=x_codes[:, c, tokens].bitcast(FP8X4),
+                    rhs_scale=x_scales[:, c, tokens],
+                    start=(c == 0),
+                    stop=(c == PASSES - 1),
+                )
+            if (gate, column_tile) not in column_tiles:
+                by_column = columns.tile([P, TOKENS], F32, tag="column")
+                column_tiles[gate, column_tile] = by_column
+            i = FLIPPED.index(gate)
+            nc.scalar.activation(
+                out=column_tiles[gate, column_tile][:, tokens], in_=acc[:, tokens],
+                func={"I": ACT.Identity, "Z": ACT.Tanh, "O": ACT.Exp}[gate],
+                bias=column_bias[:, i, column_tile : column_tile + 1], scale=(-1.0 if gate == "O" else 1.0),
+            )
+
+        def back(gate, unit):
+            if not valid(unit):
+                return
+            chunk, t = divmod(unit, TOKEN_TILES)
+            by_token_ps = psum.tile([P, CHUNK], F32, tag="back", bufs=4)
+            for k in range(TILES_PER_CHUNK):
+                nc.tensor.transpose(
+                    by_token_ps[:, k * P : (k + 1) * P],
+                    column_tiles[gate, chunk * TILES_PER_CHUNK + k][:, t * P : (t + 1) * P],
+                    ident[:],
+                )
+            live[gate, unit] = by_token_ps
+
+        def stabiliser_bias(unit):
+            t, cols = place(unit)
+            acc = psum.tile([P, CHUNK], F32, tag="group")
+            nc.tensor.matmul(out=acc[:], lhsT=ident_bf[:], rhs=mi_sb[:, t, cols], start=True, stop=False)
+            nc.tensor.matmul(out=acc[:], lhsT=ones[:], rhs=bias_rows[:, cols], start=False, stop=True)
+            nc.scalar.copy(out=f_pre[:, unit, :], in_=acc[:])
+
+        def forget_matmuls(unit):
             if not valid(unit):
                 return
             t, cols = place(unit)
             tokens = slice(t * P, (t + 1) * P)
-            for gate in ("I", "F"):
-                acc = psum.tile([P, CHUNK], F32, tag="if", bufs=4)
-                for c in range(PASSES):
-                    nc.tensor.matmul_mx(
-                        out=acc[:],
-                        lhsT=x_codes[:, c, tokens].bitcast(FP8X4),
-                        lhsT_scale=x_scales[:, c, tokens],
-                        rhs=codes[gate][:, c, cols].bitcast(FP8X4),
-                        rhs_scale=planes[gate][plane_offset[gate] : P, c, cols],
-                        start=(c == 0),
-                        stop=(c == PASSES - 1),
-                    )
-                live[gate, unit] = acc
-
-        def flip_tanh_biases():
-            nc.vector.tensor_tensor(out=tanh_rows[:], in0=tanh_w_rows[:], in1=tanh_r_rows[:], op=ALU.add)
-            flipped = psum.tile([P, P], F32, tag="tanh_out")
-            nc.tensor.transpose(flipped[:], tanh_rows[:], ident[:])
-            nc.vector.tensor_copy(out=tanh_bias[:, 0, :], in_=flipped[:, 0:COLUMN_TILES])
-            nc.vector.tensor_scalar(
-                out=tanh_bias[:, 1, :], in0=flipped[:, COLUMN_TILES : 2 * COLUMN_TILES],
-                scalar1=0.5, scalar2=None, op0=ALU.mult,
-            )
-
-        def tanh_group(group):
-            if not 0 <= group < TANH_GROUPS:
-                return
-            chunk, rest = divmod(group, GROUPS_PER_CHUNK)
-            which, quarter = divmod(rest, CHUNK // P)
-            gate = TANH_GATES[which]
-            column_tile = chunk * (CHUNK // P) + quarter
-            cols = slice(column_tile * P, (column_tile + 1) * P)
-            acc = psum.tile([P, TOKENS], F32, tag="tanh_in")
+            acc = psum.tile([P, CHUNK], F32, tag="f")
             for c in range(PASSES):
                 nc.tensor.matmul_mx(
                     out=acc[:],
-                    lhsT=codes[gate][:, c, cols].bitcast(FP8X4),
-                    lhsT_scale=planes[gate][plane_offset[gate] : P, c, cols],
-                    rhs=x_codes[:, c, :].bitcast(FP8X4),
-                    rhs_scale=x_scales[:, c, :],
+                    lhsT=x_codes[:, c, tokens].bitcast(FP8X4),
+                    lhsT_scale=x_scales[:, c, tokens],
+                    rhs=codes["F"][:, c, cols].bitcast(FP8X4),
+                    rhs_scale=planes["F"][4 * c : P, cols],
                     start=(c == 0),
                     stop=(c == PASSES - 1),
                 )
-            by_column = work.tile([P, TOKENS], F32, bufs=TANH_GROUPS)
-            nc.scalar.activation(
-                out=by_column[:], in_=acc[:], func=ACT.Tanh,
-                bias=tanh_bias[:, which, column_tile : column_tile + 1], scale=(1.0 if gate == "Z" else 0.5),
-            )
-            live[gate, "column tile", column_tile] = by_column
-
-        def back_transposes(unit):
-            if not valid(unit):
-                return
-            chunk, t = divmod(unit, TOKEN_TILES)
-            for gate in TANH_GATES:
-                by_token_ps = psum.tile([P, CHUNK], F32, tag="tanh_out")
-                for quarter in range(CHUNK // P):
-                    nc.tensor.transpose(
-                        by_token_ps[:, quarter * P : (quarter + 1) * P],
-                        live[gate, "column tile", chunk * (CHUNK // P) + quarter][:, t * P : (t + 1) * P],
-                        ident[:],
-                    )
-                live[gate, unit] = by_token_ps
-
-        def input_gate(unit):
-            if valid(unit):
-                t, cols = place(unit)
-                nc.vector.tensor_tensor(
-                    out=new_tile("i_pre", unit, 1)[:], in0=live["I", unit][:],
-                    in1=bias_all[:, GATES.index("I"), cols], op=ALU.add,
-                )
+            live["F", unit] = acc
 
         def forget_gate(unit):
             if valid(unit):
-                t, cols = place(unit)
                 nc.vector.tensor_tensor(
-                    out=new_tile("f_pre", unit, 1)[:], in0=live["F", unit][:], in1=mi_bias[:, t, cols], op=ALU.add
+                    out=f_pre[:, unit, :], in0=live["F", unit][:], in1=f_pre[:, unit, :], op=ALU.add
                 )
 
         def difference(unit):
             if valid(unit):
-                nc.vector.tensor_tensor(
-                    out=new_tile("d", unit, 2)[:], in0=live["f_pre", unit][:], in1=live["i_pre", unit][:], op=ALU.subtract
-                )
+                d = rotate.tile([P, CHUNK], F32, tag="d")
+                nc.vector.tensor_tensor(out=d[:], in0=f_pre[:, unit, :], in1=live["I", unit][:], op=ALU.subtract)
+                live["d", unit] = d
 
         def stabiliser(unit):
             if valid(unit):
                 t, cols = place(unit)
-                m_t = new_tile("m_t", unit, 3)
-                nc.vector.tensor_tensor(out=m_t[:], in0=live["f_pre", unit][:], in1=live["i_pre", unit][:], op=ALU.max)
+                m_t = rotate.tile([P, CHUNK], F32, tag="m_t")
+                nc.vector.tensor_tensor(out=m_t[:], in0=f_pre[:, unit, :], in1=live["I", unit][:], op=ALU.max)
                 nc.gpsimd.dma_start(out=m_out[:, t, cols], in_=m_t[:])
 
         def exponentials(unit):
             if valid(unit):
                 d = live["d", unit]
-                nc.scalar.activation(out=new_tile("e_i", unit, CELL_LAG + 1)[:], in_=d[:], func=ACT.Exp, scale=-1.0)
-                nc.scalar.activation(out=d[:], in_=d[:], func=ACT.Exp)
+                nc.scalar.activation(out=g[:, unit, :], in_=d[:], func=ACT.Exp)
+                nc.scalar.activation(out=e_i[:, unit, :], in_=d[:], func=ACT.Exp, scale=-1.0)
 
         def blend_factor(unit):
             if valid(unit):
                 t, cols = place(unit)
                 nc.scalar.activation(
-                    out=new_tile("g", unit, CELL_LAG + 1)[:], in_=live["d", unit][:], func=ACT.Identity,
+                    out=g[:, unit, :], in_=g[:, unit, :], func=ACT.Identity,
                     scale=m_floor[:, t : t + 1], bias=one_minus_m[:, t : t + 1],
                 )
 
@@ -346,97 +339,132 @@ def tile_customlstmcell_kernel(
             if valid(unit):
                 t, cols = place(unit)
                 nc.vector.scalar_tensor_tensor(
-                    out=new_tile("n_t", unit, LN_GROUP + RECIPROCAL_LAG)[:], in0=live["d", unit][:], scalar=1.0,
-                    in1=ni_sb[:, t, cols], op0=ALU.min, op1=ALU.mult,
+                    out=n_t[:, unit, :], in0=g[:, unit, :], scalar=1.0, in1=ni_sb[:, t, cols],
+                    op0=ALU.min, op1=ALU.mult,
                 )
 
         def normaliser(unit):
             if valid(unit):
                 t, cols = place(unit)
-                n_t = live["n_t", unit]
                 nc.vector.scalar_tensor_tensor(
-                    out=n_t[:], in0=live["e_i", unit][:], scalar=1.0, in1=n_t[:], op0=ALU.min, op1=ALU.add
+                    out=n_t[:, unit, :], in0=e_i[:, unit, :], scalar=1.0, in1=n_t[:, unit, :],
+                    op0=ALU.min, op1=ALU.add,
                 )
-                nc.gpsimd.dma_start(out=n_out[:, t, cols], in_=n_t[:])
-
-        def reciprocals(last):
-            if valid(last) and last % LN_GROUP == LN_GROUP - 1:
-                units = range(last - LN_GROUP + 1, last + 1)
-                for unit in units:
-                    nc.scalar.activation(out=new_tile("r", unit, 2 * LN_GROUP)[:], in_=live["n_t", unit][:], func=ACT.Ln)
-                for unit in units:
-                    nc.scalar.activation(out=live["r", unit][:], in_=live["r", unit][:], func=ACT.Exp, scale=-1.0)
+                nc.gpsimd.dma_start(out=n_out[:, t, cols], in_=n_t[:, unit, :])
 
         def kept_cell(unit):
             if valid(unit):
                 t, cols = place(unit)
                 nc.vector.scalar_tensor_tensor(
-                    out=new_tile("kept", unit, 1)[:], in0=live["g", unit][:], scalar=1.0, in1=ci_sb[:, t, cols],
+                    out=g[:, unit, :], in0=g[:, unit, :], scalar=1.0, in1=ci_sb[:, t, cols],
                     op0=ALU.min, op1=ALU.mult,
                 )
 
         def fresh_cell(unit):
             if valid(unit):
                 nc.vector.scalar_tensor_tensor(
-                    out=new_tile("fresh", unit, 1)[:], in0=live["e_i", unit][:], scalar=1.0, in1=live["Z", unit][:],
+                    out=e_i[:, unit, :], in0=e_i[:, unit, :], scalar=1.0, in1=live["Z", unit][:],
                     op0=ALU.min, op1=ALU.mult,
                 )
 
         def cell(unit):
             if valid(unit):
                 t, cols = place(unit)
-                c_t = new_tile("c_t", unit, 3)
                 nc.vector.scalar_tensor_tensor(
-                    out=c_t[:], in0=live["fresh", unit][:], scalar=m_f32[:, t : t + 1], in1=live["kept", unit][:],
+                    out=g[:, unit, :], in0=e_i[:, unit, :], scalar=m_f32[:, t : t + 1], in1=g[:, unit, :],
                     op0=ALU.mult, op1=ALU.add,
                 )
-                nc.sync.dma_start(out=c_out[:, t, cols], in_=c_t[:])
+                nc.sync.dma_start(out=c_out[:, t, cols], in_=g[:, unit, :])
 
-        def gated_cell(unit):
+        def divisor(unit):
             if valid(unit):
                 nc.vector.scalar_tensor_tensor(
-                    out=new_tile("oc", unit, 2)[:], in0=live["O", unit][:], scalar=1.0, in1=live["c_t", unit][:],
+                    out=n_t[:, unit, :], in0=live["O", unit][:], scalar=1.0, in1=n_t[:, unit, :],
                     op0=ALU.add, op1=ALU.mult,
                 )
+
+        def reciprocal(unit):
+            if valid(unit):
+                nc.scalar.activation(out=n_t[:, unit, :], in_=n_t[:, unit, :], func=ACT.Abs_reciprocal_sqrt)
+                nc.scalar.activation(out=n_t[:, unit, :], in_=n_t[:, unit, :], func=ACT.Square)
 
         def normalised_cell(unit):
             if valid(unit):
                 t, cols = place(unit)
-                r = live["r", unit]
                 nc.vector.scalar_tensor_tensor(
-                    out=r[:], in0=live["oc", unit][:], scalar=half_m[:, t : t + 1], in1=r[:], op0=ALU.mult, op1=ALU.mult
+                    out=n_t[:, unit, :], in0=g[:, unit, :], scalar=m_f32[:, t : t + 1], in1=n_t[:, unit, :],
+                    op0=ALU.mult, op1=ALU.mult,
                 )
 
         def hidden(unit):
             if valid(unit):
                 t, cols = place(unit)
-                r = live["r", unit]
                 nc.vector.scalar_tensor_tensor(
-                    out=r[:], in0=hi_sb[:, t, cols], scalar=one_minus_m[:, t : t + 1], in1=r[:], op0=ALU.mult, op1=ALU.add
+                    out=n_t[:, unit, :], in0=hi_sb[:, t, cols], scalar=one_minus_m[:, t : t + 1],
+                    in1=n_t[:, unit, :], op0=ALU.mult, op1=ALU.add,
                 )
-                nc.sync.dma_start(out=h_out[:, t, cols], in_=r[:])
+                nc.sync.dma_start(out=h_out[:, t, cols], in_=n_t[:, unit, :])
 
-        if_matmuls(0)
-        if_matmuls(1)
-        for step in range(UNITS + HIDDEN_LAG):
-            input_gate(step)
+        halves = (slice(0, HALF), slice(HALF, TOKENS))
+        prepare_m()
+        for k in range(TILES_PER_CHUNK):
+            column_group("I", k, halves[0])
+        stabiliser_bias(0)
+        forget_matmuls(0)
+        back("I", 0)
+        stabiliser_bias(1)
+        forget_matmuls(1)
+        back("I", 1)
+        for step in range(UNITS + 1):
             forget_gate(step)
             forgotten_n(step - 1)
             difference(step)
             normaliser(step - 1)
             stabiliser(step)
-            if_matmuls(step + 2)
-            if step == TANH_FIRST_STEP:
-                flip_tanh_biases()
             exponentials(step)
-            tanh_group(TANH_GROUPS_PER_STEP * (step - TANH_FIRST_STEP))
-            blend_factor(step)
-            tanh_group(TANH_GROUPS_PER_STEP * (step - TANH_FIRST_STEP) + 1)
-            reciprocals(step - RECIPROCAL_LAG)
-            kept_cell(step - CELL_LAG)
-            fresh_cell(step - CELL_LAG)
-            normalised_cell(step - HIDDEN_LAG)
-            cell(step - CELL_LAG)
-            hidden(step - HIDDEN_LAG)
-            gated_cell(step - CELL_LAG)
-            back_transposes(step - CELL_LAG + 1)
+            if step == 0:
+                for k in range(TILES_PER_CHUNK):
+                    column_group("I", k, halves[1])
+            if step == 3:
+                column_group("I", 7)
+                back("I", 4)
+            if step + 2 < UNITS:
+                stabiliser_bias(step + 2)
+            forget_matmuls(step + 2)
+            if step != 2:
+                back("I", step + 2)
+            if step in (0, 1, 2):
+                column_group("I", TILES_PER_CHUNK + step)
+            if step == 2:
+                flipped_zo = flip_biases("ZO")
+            if step == 3:
+                finish_biases("ZO", flipped_zo)
+            if step in (4, 5, 6, 7):
+                column_group("Z", step - 4)
+            if step in (5, 6, 7, 8):
+                blend_factor(step - 5)
+        back("Z", 0)
+        back("Z", 1)
+        kept_cell(0)
+        for step in range(UNITS):
+            fresh_cell(step)
+            kept_cell(step + 1)
+            cell(step)
+            if step < 2:
+                column_group("Z", TILES_PER_CHUNK + 2 * step)
+                column_group("Z", TILES_PER_CHUNK + 2 * step + 1)
+            back("Z", step + 2)
+            if 1 <= step < 5:
+                blend_factor(step + 3)
+            if step >= 2:
+                column_group("O", step - 2)
+        column_group("O", 6)
+        column_group("O", 7)
+        back("O", 0)
+        back("O", 1)
+        for step in range(UNITS + 4):
+            divisor(step)
+            normalised_cell(step - 3)
+            hidden(step - 4)
+            back("O", step + 2)
+            reciprocal(step)

@@ -78,6 +78,7 @@ def tile_customlstmcell_kernel(
         ident_bf = keep.tile([P, P], BF16)
         ones = keep.tile([P, P], BF16)
         bias_rows = keep.tile([P, DFF], BF16)
+        bias_f = keep.tile([P, CHUNK], F32)
         w_rows, r_rows, sum_rows = {}, {}, {}
         for name in ("I", "ZO"):
             w_tile = keep.tile([P, P], BF16, name="w_rows_" + name)
@@ -99,10 +100,10 @@ def tile_customlstmcell_kernel(
             grouped.append(grouped_k)
 
         make_identity(nc, ident[:])
-        for gate in ("I", "F"):
-            nc.vector.memset(planes[gate][:].bitcast(I32), 0)
         nc.vector.memset(w_rows["I"][:], 0.0)
         nc.vector.memset(r_rows["I"][:], 0.0)
+        for gate in ("I", "F"):
+            nc.vector.memset(planes[gate][:].bitcast(I32), 0)
         nc.vector.memset(bias_rows[:].bitcast(I32), 0)
         for gate in ("Z", "O"):
             nc.vector.memset(planes[gate][:].bitcast(I32), 0)
@@ -144,23 +145,24 @@ def tile_customlstmcell_kernel(
                 queue.dma_start(out=w_rows[name][rows, :], in_=w_bias[gate].rearrange("(i n) -> i n", n=P))
                 queue.dma_start(out=r_rows[name][rows, :], in_=r_bias[gate].rearrange("(i n) -> i n", n=P))
 
-        load_scales("I", (0, 1, 2))
-        for half in range(2):
+        def load_x(half, queue):
             tiles = slice(2 * half, 2 * half + 2)
-            nc.sync.dma_start(out=hi_sb[:, tiles, :], in_=by_token(Hi)[:, tiles, :])
-            nc.sync.dma_start(out=zi_sb[:, tiles, :], in_=by_token(Zi)[:, tiles, :])
-        load_scales("I", (3,))
-        load_scales("F", (0, 1))
-        load_codes("I", 0)
-        load_scales("F", (2, 3))
-        load_codes("F", 0)
-        nc.sync.dma_start(out=mi_sb[:, :, 0:CHUNK], in_=by_token(Mi)[:, :, 0:CHUNK])
-        load_column_biases(nc.gpsimd, "I")
+            queue.dma_start(out=hi_sb[:, tiles, :], in_=by_token(Hi)[:, tiles, :])
+            queue.dma_start(out=zi_sb[:, tiles, :], in_=by_token(Zi)[:, tiles, :])
+
         nc.gpsimd.dma_start(out=bias_rows[0:1, :], in_=w_bias["F"].unsqueeze(0))
         nc.gpsimd.dma_start(out=bias_rows[1:2, :], in_=r_bias["F"].unsqueeze(0))
         nc.gpsimd.dma_start(
             out=m_bf[:], in_=m.flatten_outer_dims().rearrange("(p t) o -> p (t o)", t=TOKEN_TILES)
         )
+        load_x(0, nc.sync)
+        nc.sync.dma_start(out=mi_sb[:, :, 0:CHUNK], in_=by_token(Mi)[:, :, 0:CHUNK])
+        load_scales("F")
+        load_codes("F", 0)
+        load_column_biases(nc.sync, "I")
+        load_x(1, nc.sync)
+        load_scales("I")
+        load_codes("I", 0)
         load_column_biases(nc.gpsimd, "ZO")
         nc.sync.dma_start(out=ni_sb[:], in_=by_token(Ni))
         load_codes("I", 1)
@@ -181,7 +183,7 @@ def tile_customlstmcell_kernel(
             piece = half * PASSES + c
             x_words = x_sb[:].bitcast(F32)
             out_words = grouped[piece][:].bitcast(F32).rearrange("p (r u) -> p r u", u=2)
-            xt = psum.tile([P, 2, 2 * P], F32, tag=("back" if piece % 3 else "f"), bufs=(4 if piece % 3 else 2))
+            xt = psum.tile([P, 2, 2 * P], F32, tag=("back" if piece % 3 else "f"), bufs=(3 if piece % 3 else 2))
             for u in range(2):
                 for s in range(2):
                     nc.tensor.transpose(
@@ -201,7 +203,7 @@ def tile_customlstmcell_kernel(
 
         def flip_biases(name):
             nc.vector.tensor_tensor(out=sum_rows[name][:], in0=w_rows[name][:], in1=r_rows[name][:], op=ALU.add)
-            flipped = psum.tile([P, P], F32, tag="back", bufs=4)
+            flipped = psum.tile([P, P], F32, tag="back", bufs=3)
             nc.tensor.transpose(flipped[:], sum_rows[name][:], ident[:])
             return flipped
 
@@ -213,20 +215,10 @@ def tile_customlstmcell_kernel(
                     scalar1=(-1.0 if gate == "O" else 1.0), scalar2=None, op0=ALU.mult,
                 )
 
-        transpose_piece(0, 0)
-        transpose_piece(0, 1)
-        transpose_piece(0, 2)
-        quantise_piece(0, 0)
-        quantise_piece(0, 1)
-        quantise_piece(0, 2)
-        flipped_i = flip_biases("I")
-        transpose_piece(1, 0)
-        transpose_piece(1, 1)
-        finish_biases("I", flipped_i)
-        quantise_piece(1, 0)
-        transpose_piece(1, 2)
-        quantise_piece(1, 1)
-        quantise_piece(1, 2)
+        for c in range(PASSES):
+            transpose_piece(0, c)
+        for c in range(PASSES):
+            quantise_piece(0, c)
 
         column_tiles = {}
         live = {}
@@ -243,7 +235,7 @@ def tile_customlstmcell_kernel(
 
         def column_group(gate, column_tile, tokens=slice(0, TOKENS)):
             cols = slice(column_tile * P, (column_tile + 1) * P)
-            acc = psum.tile([P, TOKENS], F32, tag="group")
+            acc = psum.tile([P, TOKENS], F32, tag="group", bufs=3)
             for c in range(PASSES):
                 nc.tensor.matmul_mx(
                     out=acc[:, tokens],
@@ -268,7 +260,7 @@ def tile_customlstmcell_kernel(
             if not valid(unit):
                 return
             chunk, t = divmod(unit, TOKEN_TILES)
-            by_token_ps = psum.tile([P, CHUNK], F32, tag="back", bufs=4)
+            by_token_ps = psum.tile([P, CHUNK], F32, tag=("f" if gate == "O" else "back"), bufs=(2 if gate == "O" else 3))
             for k in range(TILES_PER_CHUNK):
                 nc.tensor.transpose(
                     by_token_ps[:, k * P : (k + 1) * P],
@@ -279,10 +271,19 @@ def tile_customlstmcell_kernel(
 
         def stabiliser_bias(unit):
             t, cols = place(unit)
-            acc = psum.tile([P, CHUNK], F32, tag="group")
+            acc = psum.tile([P, CHUNK], F32, tag="group", bufs=3)
             nc.tensor.matmul(out=acc[:], lhsT=ident_bf[:], rhs=mi_sb[:, t, cols], start=True, stop=False)
             nc.tensor.matmul(out=acc[:], lhsT=ones[:], rhs=bias_rows[:, cols], start=False, stop=True)
             nc.scalar.copy(out=f_pre[:, unit, :], in_=acc[:])
+
+        def spread_bias():
+            acc = psum.tile([P, CHUNK], F32, tag="group", bufs=3)
+            nc.tensor.matmul(out=acc[:], lhsT=ones[:], rhs=bias_rows[:, 0:CHUNK], start=True, stop=True)
+            nc.scalar.copy(out=bias_f[:], in_=acc[:])
+
+        def early_stabiliser_bias(unit):
+            t, cols = place(unit)
+            nc.vector.tensor_tensor(out=f_pre[:, unit, :], in0=mi_sb[:, t, cols], in1=bias_f[:], op=ALU.add)
 
         def forget_matmuls(unit):
             if not valid(unit):
@@ -405,44 +406,57 @@ def tile_customlstmcell_kernel(
                 )
                 nc.sync.dma_start(out=h_out[:, t, cols], in_=n_t[:, unit, :])
 
+        JOBS = [[("Z", 6), ("Z", 7)], [("O", 0), ("O", 1)], [("O", 2)], [("O", 3), ("O", 4)], [("O", 5)], [("O", 6), ("O", 7)], [], []]
         halves = (slice(0, HALF), slice(HALF, TOKENS))
+        spread_bias()
+        for unit in range(2):
+            early_stabiliser_bias(unit)
+            forget_matmuls(unit)
+            forget_gate(unit)
+        for c in range(PASSES):
+            transpose_piece(1, c)
+        flipped_i = flip_biases("I")
+        quantise_piece(1, 0)
+        finish_biases("I", flipped_i)
+        quantise_piece(1, 1)
+        quantise_piece(1, 2)
+        early_stabiliser_bias(2)
+        early_stabiliser_bias(3)
         prepare_m()
         for k in range(TILES_PER_CHUNK):
             column_group("I", k, halves[0])
-        stabiliser_bias(0)
-        forget_matmuls(0)
         back("I", 0)
-        stabiliser_bias(1)
-        forget_matmuls(1)
+        forget_matmuls(2)
         back("I", 1)
+        column_group("I", 0, halves[1])
+        column_group("I", 1, halves[1])
         for step in range(UNITS + 1):
-            forget_gate(step)
             forgotten_n(step - 1)
             difference(step)
             normaliser(step - 1)
             stabiliser(step)
+            forget_gate(step + 2)
             exponentials(step)
             if step == 0:
-                for k in range(TILES_PER_CHUNK):
-                    column_group("I", k, halves[1])
-            if step == 3:
-                column_group("I", 7)
-                back("I", 4)
-            if step + 2 < UNITS:
-                stabiliser_bias(step + 2)
-            forget_matmuls(step + 2)
-            if step != 2:
-                back("I", step + 2)
-            if step in (0, 1, 2):
-                column_group("I", TILES_PER_CHUNK + step)
-            if step == 2:
+                column_group("I", 2, halves[1])
+                column_group("I", 3, halves[1])
+            if 1 <= step < 5:
+                stabiliser_bias(step + 3)
+            forget_matmuls(step + 3)
+            if step in (1, 2):
+                column_group("I", 2 * step + 2)
+                column_group("I", 2 * step + 3)
+            back("I", step + 2)
+            if step == 1:
                 flipped_zo = flip_biases("ZO")
             if step == 3:
                 finish_biases("ZO", flipped_zo)
             if step in (4, 5, 6, 7):
                 column_group("Z", step - 4)
-            if step in (5, 6, 7, 8):
-                blend_factor(step - 5)
+        column_group("Z", 4)
+        blend_factor(0)
+        blend_factor(1)
+        column_group("Z", 5)
         back("Z", 0)
         back("Z", 1)
         kept_cell(0)
@@ -450,21 +464,16 @@ def tile_customlstmcell_kernel(
             fresh_cell(step)
             kept_cell(step + 1)
             cell(step)
-            if step < 2:
-                column_group("Z", TILES_PER_CHUNK + 2 * step)
-                column_group("Z", TILES_PER_CHUNK + 2 * step + 1)
+            divisor(step - 5)
+            blend_factor(step + 2)
+            for gate, k in JOBS[step]:
+                column_group(gate, k)
             back("Z", step + 2)
-            if 1 <= step < 5:
-                blend_factor(step + 3)
-            if step >= 2:
-                column_group("O", step - 2)
-        column_group("O", 6)
-        column_group("O", 7)
-        back("O", 0)
-        back("O", 1)
-        for step in range(UNITS + 4):
-            divisor(step)
-            normalised_cell(step - 3)
-            hidden(step - 4)
-            back("O", step + 2)
-            reciprocal(step)
+            back("O", step - 4)
+            reciprocal(step - 5)
+        for step in range(UNITS + 2):
+            divisor(step + 3)
+            normalised_cell(step)
+            hidden(step - 1)
+            back("O", step + 4)
+            reciprocal(step + 3)

@@ -78,7 +78,7 @@ def tile_customlstmcell_kernel(
         ident_bf = keep.tile([P, P], BF16)
         ones = keep.tile([P, P], BF16)
         bias_rows = keep.tile([P, DFF], BF16)
-        bias_f = keep.tile([P, CHUNK], F32)
+        bias_f = keep.tile([P, DFF], F32)
         w_rows, r_rows, sum_rows = {}, {}, {}
         for name in ("I", "ZO"):
             w_tile = keep.tile([P, P], BF16, name="w_rows_" + name)
@@ -163,18 +163,14 @@ def tile_customlstmcell_kernel(
         load_x(1, nc.sync)
         load_scales("I")
         load_codes("I", 0)
-        load_column_biases(nc.gpsimd, "ZO")
-        nc.sync.dma_start(out=ni_sb[:], in_=by_token(Ni))
-        load_codes("I", 1)
         nc.sync.dma_start(out=mi_sb[:, :, CHUNK:DFF], in_=by_token(Mi)[:, :, CHUNK:DFF])
         load_codes("F", 1)
+        load_codes("I", 1)
+        nc.sync.dma_start(out=ni_sb[:], in_=by_token(Ni))
         load_scales("Z")
         load_codes("Z", 0)
         load_codes("Z", 1)
-        nc.sync.dma_start(out=ci_sb[:], in_=by_token(Ci))
-        load_scales("O")
-        load_codes("O", 0)
-        load_codes("O", 1)
+        load_column_biases(nc.gpsimd, "ZO")
 
         x_blocks = ((hi_sb, 0), (hi_sb, 1), (zi_sb, 0))
 
@@ -183,7 +179,7 @@ def tile_customlstmcell_kernel(
             piece = half * PASSES + c
             x_words = x_sb[:].bitcast(F32)
             out_words = grouped[piece][:].bitcast(F32).rearrange("p (r u) -> p r u", u=2)
-            xt = psum.tile([P, 2, 2 * P], F32, tag=("back" if piece % 3 else "f"), bufs=(3 if piece % 3 else 2))
+            xt = psum.tile([P, 2, 2 * P], F32, tag=("group" if half else "back"), bufs=3)
             for u in range(2):
                 for s in range(2):
                     nc.tensor.transpose(
@@ -191,7 +187,7 @@ def tile_customlstmcell_kernel(
                         x_words[:, 2 * half + s, 256 * group + u : 256 * (group + 1) : 2],
                         ident[:],
                     )
-            copy = nc.vector.tensor_copy if piece % 2 == 0 else nc.scalar.copy
+            copy = nc.vector.tensor_copy if piece in (0, 2) else nc.scalar.copy
             copy(out=out_words, in_=xt[:].rearrange("p u r -> p r u"))
 
         def quantise_piece(half, c):
@@ -201,18 +197,20 @@ def tile_customlstmcell_kernel(
                 in_=grouped[half * PASSES + c][:],
             )
 
+        def sum_biases(name):
+            nc.gpsimd.tensor_tensor(out=sum_rows[name][:], in0=w_rows[name][:], in1=r_rows[name][:], op=ALU.add)
+
         def flip_biases(name):
-            nc.vector.tensor_tensor(out=sum_rows[name][:], in0=w_rows[name][:], in1=r_rows[name][:], op=ALU.add)
             flipped = psum.tile([P, P], F32, tag="back", bufs=3)
             nc.tensor.transpose(flipped[:], sum_rows[name][:], ident[:])
             return flipped
 
         def finish_biases(name, flipped):
             for i, gate in enumerate(name):
-                nc.vector.tensor_scalar(
+                nc.scalar.activation(
                     out=column_bias[:, FLIPPED.index(gate), :],
-                    in0=flipped[:, i * COLUMN_TILES : (i + 1) * COLUMN_TILES],
-                    scalar1=(-1.0 if gate == "O" else 1.0), scalar2=None, op0=ALU.mult,
+                    in_=flipped[:, i * COLUMN_TILES : (i + 1) * COLUMN_TILES],
+                    func=ACT.Copy, scale=(-1.0 if gate == "O" else 1.0),
                 )
 
         for c in range(PASSES):
@@ -227,9 +225,9 @@ def tile_customlstmcell_kernel(
             return 0 <= unit < UNITS
 
         def prepare_m():
-            nc.vector.tensor_copy(out=m_f32[:], in_=m_bf[:])
-            nc.vector.tensor_scalar(out=m_floor[:], in0=m_bf[:], scalar1=SMALLEST_NORMAL, scalar2=None, op0=ALU.max)
-            nc.vector.tensor_scalar(
+            nc.gpsimd.tensor_copy(out=m_f32[:], in_=m_bf[:])
+            nc.gpsimd.tensor_scalar(out=m_floor[:], in0=m_bf[:], scalar1=SMALLEST_NORMAL, scalar2=None, op0=ALU.max)
+            nc.gpsimd.tensor_scalar(
                 out=one_minus_m[:], in0=m_bf[:], scalar1=-1.0, scalar2=1.0, op0=ALU.mult, op1=ALU.add
             )
 
@@ -269,21 +267,17 @@ def tile_customlstmcell_kernel(
                 )
             live[gate, unit] = by_token_ps
 
-        def stabiliser_bias(unit):
-            t, cols = place(unit)
-            acc = psum.tile([P, CHUNK], F32, tag="group", bufs=3)
-            nc.tensor.matmul(out=acc[:], lhsT=ident_bf[:], rhs=mi_sb[:, t, cols], start=True, stop=False)
-            nc.tensor.matmul(out=acc[:], lhsT=ones[:], rhs=bias_rows[:, cols], start=False, stop=True)
-            nc.scalar.copy(out=f_pre[:, unit, :], in_=acc[:])
-
         def spread_bias():
-            acc = psum.tile([P, CHUNK], F32, tag="group", bufs=3)
-            nc.tensor.matmul(out=acc[:], lhsT=ones[:], rhs=bias_rows[:, 0:CHUNK], start=True, stop=True)
-            nc.scalar.copy(out=bias_f[:], in_=acc[:])
+            for chunk in range(CHUNKS):
+                cols = slice(chunk * CHUNK, (chunk + 1) * CHUNK)
+                acc = psum.tile([P, CHUNK], F32, tag="group", bufs=3)
+                nc.tensor.matmul(out=acc[:], lhsT=ones[:], rhs=bias_rows[:, cols], start=True, stop=True)
+                nc.scalar.copy(out=bias_f[:, cols], in_=acc[:])
 
         def early_stabiliser_bias(unit):
             t, cols = place(unit)
-            nc.vector.tensor_tensor(out=f_pre[:, unit, :], in0=mi_sb[:, t, cols], in1=bias_f[:], op=ALU.add)
+            engine = nc.vector if unit < TOKEN_TILES else nc.gpsimd
+            engine.tensor_tensor(out=f_pre[:, unit, :], in0=mi_sb[:, t, cols], in1=bias_f[:, cols], op=ALU.add)
 
         def forget_matmuls(unit):
             if not valid(unit):
@@ -318,9 +312,10 @@ def tile_customlstmcell_kernel(
         def stabiliser(unit):
             if valid(unit):
                 t, cols = place(unit)
-                m_t = rotate.tile([P, CHUNK], F32, tag="m_t")
-                nc.vector.tensor_tensor(out=m_t[:], in0=f_pre[:, unit, :], in1=live["I", unit][:], op=ALU.max)
-                nc.gpsimd.dma_start(out=m_out[:, t, cols], in_=m_t[:])
+                nc.vector.tensor_tensor(
+                    out=f_pre[:, unit, :], in0=f_pre[:, unit, :], in1=live["I", unit][:], op=ALU.max
+                )
+                nc.sync.dma_start(out=m_out[:, t, cols], in_=f_pre[:, unit, :])
 
         def exponentials(unit):
             if valid(unit):
@@ -406,57 +401,66 @@ def tile_customlstmcell_kernel(
                 )
                 nc.sync.dma_start(out=h_out[:, t, cols], in_=n_t[:, unit, :])
 
+        A_JOBS = {0: (("I", 4),), 1: (("I", 5),), 2: (("I", 6), ("I", 7)), 4: (("Z", 0),), 5: (("Z", 1),), 6: (("Z", 2),), 7: (("Z", 3),), 8: (("Z", 4),), 9: (("Z", 5),)}
+        I_BACKS = {0: (2,), 1: (3,), 2: (4,), 3: (5,), 4: (6,), 5: (7,)}
         JOBS = [[("Z", 6), ("Z", 7)], [("O", 0), ("O", 1)], [("O", 2)], [("O", 3), ("O", 4)], [("O", 5)], [("O", 6), ("O", 7)], [], []]
         halves = (slice(0, HALF), slice(HALF, TOKENS))
         spread_bias()
-        for unit in range(2):
+        for unit in range(TOKEN_TILES):
             early_stabiliser_bias(unit)
+        for unit in range(2):
             forget_matmuls(unit)
             forget_gate(unit)
         for c in range(PASSES):
             transpose_piece(1, c)
+        sum_biases("I")
         flipped_i = flip_biases("I")
         quantise_piece(1, 0)
         finish_biases("I", flipped_i)
         quantise_piece(1, 1)
         quantise_piece(1, 2)
-        early_stabiliser_bias(2)
-        early_stabiliser_bias(3)
         prepare_m()
+        sum_biases("ZO")
+        for unit in (2, 3):
+            forget_matmuls(unit)
+            forget_gate(unit)
         for k in range(TILES_PER_CHUNK):
             column_group("I", k, halves[0])
         back("I", 0)
-        forget_matmuls(2)
         back("I", 1)
         column_group("I", 0, halves[1])
         column_group("I", 1, halves[1])
-        for step in range(UNITS + 1):
-            forgotten_n(step - 1)
+        column_group("I", 2, halves[1])
+        column_group("I", 3, halves[1])
+        for step in range(UNITS + 2):
+            forgotten_n(step - 2)
             difference(step)
-            normaliser(step - 1)
+            normaliser(step - 2)
             stabiliser(step)
-            forget_gate(step + 2)
-            exponentials(step)
+            forget_gate(step + 3 if step >= 1 else -1)
             if step == 0:
-                column_group("I", 2, halves[1])
-                column_group("I", 3, halves[1])
-            if 1 <= step < 5:
-                stabiliser_bias(step + 3)
-            forget_matmuls(step + 3)
-            if step in (1, 2):
-                column_group("I", 2 * step + 2)
-                column_group("I", 2 * step + 3)
-            back("I", step + 2)
+                for unit in range(TOKEN_TILES, UNITS):
+                    early_stabiliser_bias(unit)
             if step == 1:
+                nc.sync.dma_start(out=ci_sb[:], in_=by_token(Ci))
+            if step == 2:
+                load_scales("O")
+            if step == 3:
+                load_codes("O", 0)
+            if step == 4:
+                load_codes("O", 1)
+            if step == 2:
                 flipped_zo = flip_biases("ZO")
             if step == 3:
                 finish_biases("ZO", flipped_zo)
-            if step in (4, 5, 6, 7):
-                column_group("Z", step - 4)
-        column_group("Z", 4)
-        blend_factor(0)
-        blend_factor(1)
-        column_group("Z", 5)
+            for gate, k in A_JOBS.get(step, ()):
+                column_group(gate, k)
+            exponentials(step)
+            forget_matmuls(step + 4)
+            for unit in I_BACKS.get(step, ()):
+                back("I", unit)
+            if step >= UNITS:
+                blend_factor(step - UNITS)
         back("Z", 0)
         back("Z", 1)
         kept_cell(0)

@@ -78,6 +78,7 @@ def tile_customlstmcell_kernel(
         ident_bf = keep.tile([P, P], BF16)
         ones = keep.tile([P, P], BF16)
         bias_rows = keep.tile([P, DFF], BF16)
+        minus_m = keep.tile([P, TOKEN_TILES, P], BF16)
         bias_f = keep.tile([P, DFF], F32)
         w_rows, r_rows, sum_rows = {}, {}, {}
         for name in ("I", "ZO"):
@@ -100,16 +101,15 @@ def tile_customlstmcell_kernel(
             grouped.append(grouped_k)
 
         make_identity(nc, ident[:])
+        nc.vector.memset(bias_rows[:].bitcast(I32), 0)
+        nc.vector.memset(planes["F"][:].bitcast(I32), 0)
+        nc.vector.memset(ones[:], 1.0)
         nc.vector.memset(w_rows["I"][:], 0.0)
         nc.vector.memset(r_rows["I"][:], 0.0)
-        for gate in ("I", "F"):
-            nc.vector.memset(planes[gate][:].bitcast(I32), 0)
-        nc.vector.memset(bias_rows[:].bitcast(I32), 0)
-        for gate in ("Z", "O"):
+        for gate in ("I", "Z", "O"):
             nc.vector.memset(planes[gate][:].bitcast(I32), 0)
         nc.vector.memset(w_rows["ZO"][:], 0.0)
         nc.vector.memset(r_rows["ZO"][:], 0.0)
-        nc.vector.memset(ones[:], 1.0)
         nc.vector.tensor_copy(out=ident_bf[:], in_=ident[:])
 
         def place(unit):
@@ -171,6 +171,10 @@ def tile_customlstmcell_kernel(
         load_codes("Z", 0)
         load_codes("Z", 1)
         load_column_biases(nc.gpsimd, "ZO")
+        nc.sync.dma_start(out=ci_sb[:], in_=by_token(Ci))
+        load_scales("O")
+        load_codes("O", 0)
+        load_codes("O", 1)
 
         x_blocks = ((hi_sb, 0), (hi_sb, 1), (zi_sb, 0))
 
@@ -346,7 +350,7 @@ def tile_customlstmcell_kernel(
                     out=n_t[:, unit, :], in0=e_i[:, unit, :], scalar=1.0, in1=n_t[:, unit, :],
                     op0=ALU.min, op1=ALU.add,
                 )
-                nc.gpsimd.dma_start(out=n_out[:, t, cols], in_=n_t[:, unit, :])
+                nc.sync.dma_start(out=n_out[:, t, cols], in_=n_t[:, unit, :])
 
         def kept_cell(unit):
             if valid(unit):
@@ -392,6 +396,27 @@ def tile_customlstmcell_kernel(
                     op0=ALU.mult, op1=ALU.mult,
                 )
 
+        def prepare_blend():
+            for t in range(TOKEN_TILES):
+                nc.gpsimd.tensor_scalar(
+                    out=minus_m[:, t, :], in0=ident_bf[:], scalar1=m_f32[:, t : t + 1], scalar2=-1.0,
+                    op0=ALU.mult, op1=ALU.mult,
+                )
+
+        def hidden_sum(unit):
+            t, cols = place(unit)
+            acc = psum.tile([P, CHUNK], F32, tag="group", bufs=3)
+            nc.tensor.matmul(out=acc[:], lhsT=ident_bf[:], rhs=hi_sb[:, t, cols], start=True, stop=False)
+            nc.tensor.matmul(out=acc[:], lhsT=minus_m[:, t, :], rhs=hi_sb[:, t, cols], start=False, stop=False)
+            nc.tensor.matmul(out=acc[:], lhsT=ident[:], rhs=n_t[:, unit, :], start=False, stop=True)
+            live["H", unit] = acc
+
+        def hidden_copy(unit):
+            t, cols = place(unit)
+            h_t = rotate.tile([P, CHUNK], F32, tag="m_t")
+            nc.scalar.copy(out=h_t[:], in_=live["H", unit][:])
+            nc.sync.dma_start(out=h_out[:, t, cols], in_=h_t[:])
+
         def hidden(unit):
             if valid(unit):
                 t, cols = place(unit)
@@ -401,9 +426,12 @@ def tile_customlstmcell_kernel(
                 )
                 nc.sync.dma_start(out=h_out[:, t, cols], in_=n_t[:, unit, :])
 
-        A_JOBS = {0: (("I", 4),), 1: (("I", 5),), 2: (("I", 6), ("I", 7)), 4: (("Z", 0),), 5: (("Z", 1),), 6: (("Z", 2),), 7: (("Z", 3),), 8: (("Z", 4),), 9: (("Z", 5),)}
+        A_JOBS = {0: (("I", 4),), 1: (("I", 5),), 2: (("I", 6), ("I", 7)), 4: (("Z", 0), ("Z", 1)), 5: (("Z", 2),), 6: (("Z", 3), ("Z", 4)), 7: (("Z", 5),), 8: (("Z", 6), ("Z", 7)), 9: (("O", 0),)}
         I_BACKS = {0: (2,), 1: (3,), 2: (4,), 3: (5,), 4: (6,), 5: (7,)}
-        JOBS = [[("Z", 6), ("Z", 7)], [("O", 0), ("O", 1)], [("O", 2)], [("O", 3), ("O", 4)], [("O", 5)], [("O", 6), ("O", 7)], [], []]
+        BLENDS = [[2, 3], [4], [5, 6], [7], [], [], [], []]
+        SUMS = [[], [], [], [0, 1], [], [], [], [], [], []]
+        COPIES = [[], [], [], [], [], [0, 1], [], [], [], []]
+        JOBS = [[("O", 1), ("O", 2)], [("O", 3)], [("O", 4), ("O", 5)], [("O", 6)], [("O", 7)], [], [], []]
         halves = (slice(0, HALF), slice(HALF, TOKENS))
         spread_bias()
         for unit in range(TOKEN_TILES):
@@ -420,6 +448,8 @@ def tile_customlstmcell_kernel(
         quantise_piece(1, 1)
         quantise_piece(1, 2)
         prepare_m()
+        for unit in range(TOKEN_TILES, UNITS):
+            early_stabiliser_bias(unit)
         sum_biases("ZO")
         for unit in (2, 3):
             forget_matmuls(unit)
@@ -438,25 +468,19 @@ def tile_customlstmcell_kernel(
             normaliser(step - 2)
             stabiliser(step)
             forget_gate(step + 3 if step >= 1 else -1)
-            if step == 0:
-                for unit in range(TOKEN_TILES, UNITS):
-                    early_stabiliser_bias(unit)
-            if step == 1:
-                nc.sync.dma_start(out=ci_sb[:], in_=by_token(Ci))
-            if step == 2:
-                load_scales("O")
-            if step == 3:
-                load_codes("O", 0)
-            if step == 4:
-                load_codes("O", 1)
             if step == 2:
                 flipped_zo = flip_biases("ZO")
             if step == 3:
                 finish_biases("ZO", flipped_zo)
+                prepare_blend()
+            if step < 1:
+                exponentials(step)
+                forget_matmuls(step + 4)
             for gate, k in A_JOBS.get(step, ()):
                 column_group(gate, k)
-            exponentials(step)
-            forget_matmuls(step + 4)
+            if step >= 1:
+                exponentials(step)
+                forget_matmuls(step + 4)
             for unit in I_BACKS.get(step, ()):
                 back("I", unit)
             if step >= UNITS:
@@ -468,16 +492,21 @@ def tile_customlstmcell_kernel(
             fresh_cell(step)
             kept_cell(step + 1)
             cell(step)
-            divisor(step - 5)
-            blend_factor(step + 2)
+            divisor(step - 4)
+            for unit in BLENDS[step]:
+                blend_factor(unit)
             for gate, k in JOBS[step]:
                 column_group(gate, k)
             back("Z", step + 2)
-            back("O", step - 4)
-            reciprocal(step - 5)
+            back("O", step - 3)
+            reciprocal(step - 4)
         for step in range(UNITS + 2):
-            divisor(step + 3)
+            divisor(step + 4)
             normalised_cell(step)
-            hidden(step - 1)
-            back("O", step + 4)
-            reciprocal(step + 3)
+            hidden(step - 1 if step > 2 else -1)
+            back("O", step + 5)
+            reciprocal(step + 4)
+            for unit in SUMS[step]:
+                hidden_sum(unit)
+            for unit in COPIES[step]:
+                hidden_copy(unit)

@@ -77,6 +77,7 @@ def tile_customlstmcell_kernel(
         ident = keep.tile([P, P], F32)
         ident_bf = keep.tile([P, P], BF16)
         ones = keep.tile([P, P], BF16)
+        idle_rows = keep.tile([P, CHUNK], BF16)
         bias_rows = keep.tile([P, DFF], BF16)
         minus_m = keep.tile([P, TOKEN_TILES, P], BF16)
         bias_f = keep.tile([P, DFF], F32)
@@ -104,6 +105,7 @@ def tile_customlstmcell_kernel(
         nc.vector.memset(bias_rows[:].bitcast(I32), 0)
         nc.vector.memset(planes["F"][:].bitcast(I32), 0)
         nc.vector.memset(ones[:], 1.0)
+        nc.vector.memset(idle_rows[:].bitcast(I32), 0)
         nc.vector.memset(w_rows["I"][:], 0.0)
         nc.vector.memset(r_rows["I"][:], 0.0)
         for gate in ("I", "Z", "O"):
@@ -178,6 +180,11 @@ def tile_customlstmcell_kernel(
 
         x_blocks = ((hi_sb, 0), (hi_sb, 1), (zi_sb, 0))
 
+        def warm_up(count):
+            acc = psum.tile([P, CHUNK], F32, tag="group", bufs=3)
+            for k in range(count):
+                nc.tensor.matmul(out=acc[:], lhsT=ones[:], rhs=idle_rows[:], start=True, stop=True)
+
         def transpose_piece(half, c):
             x_sb, group = x_blocks[c]
             piece = half * PASSES + c
@@ -217,8 +224,10 @@ def tile_customlstmcell_kernel(
                     func=ACT.Copy, scale=(-1.0 if gate == "O" else 1.0),
                 )
 
+        warm_up(3)
         for c in range(PASSES):
             transpose_piece(0, c)
+        warm_up(4)
         for c in range(PASSES):
             quantise_piece(0, c)
 
@@ -413,24 +422,30 @@ def tile_customlstmcell_kernel(
 
         def hidden_copy(unit):
             t, cols = place(unit)
-            h_t = rotate.tile([P, CHUNK], F32, tag="m_t")
-            nc.scalar.copy(out=h_t[:], in_=live["H", unit][:])
-            nc.sync.dma_start(out=h_out[:, t, cols], in_=h_t[:])
+            nc.scalar.copy(out=n_t[:, unit, :], in_=live["H", unit][:])
+            nc.sync.dma_start(out=h_out[:, t, cols], in_=n_t[:, unit, :])
 
         def hidden(unit):
             if valid(unit):
                 t, cols = place(unit)
-                nc.vector.scalar_tensor_tensor(
-                    out=n_t[:, unit, :], in0=hi_sb[:, t, cols], scalar=one_minus_m[:, t : t + 1],
-                    in1=n_t[:, unit, :], op0=ALU.mult, op1=ALU.add,
-                )
-                nc.sync.dma_start(out=h_out[:, t, cols], in_=n_t[:, unit, :])
+                parts = 2 if unit == UNITS - 1 else 1
+                width = CHUNK // parts
+                for part in range(parts):
+                    own = slice(part * width, (part + 1) * width)
+                    cols = slice(unit // TOKEN_TILES * CHUNK + part * width, unit // TOKEN_TILES * CHUNK + (part + 1) * width)
+                    nc.vector.scalar_tensor_tensor(
+                        out=n_t[:, unit, own], in0=hi_sb[:, t, cols], scalar=one_minus_m[:, t : t + 1],
+                        in1=n_t[:, unit, own], op0=ALU.mult, op1=ALU.add,
+                    )
+                    nc.sync.dma_start(out=h_out[:, t, cols], in_=n_t[:, unit, own])
 
         A_JOBS = {0: (("I", 4),), 1: (("I", 5),), 2: (("I", 6), ("I", 7)), 4: (("Z", 0), ("Z", 1)), 5: (("Z", 2),), 6: (("Z", 3), ("Z", 4)), 7: (("Z", 5),), 8: (("Z", 6), ("Z", 7)), 9: (("O", 0),)}
         I_BACKS = {0: (2,), 1: (3,), 2: (4,), 3: (5,), 4: (6,), 5: (7,)}
         BLENDS = [[2, 3], [4], [5, 6], [7], [], [], [], []]
-        SUMS = [[], [], [], [0, 1], [], [], [], [], [], []]
-        COPIES = [[], [], [], [], [], [0, 1], [], [], [], []]
+        COPIES = {4: (2,)}
+        NORMALISED = {6: (0, 1), 7: (2,)}
+        DIVISORS = {4: (0, 1), 5: (2, 3), 6: (4, 5), 7: (6, 7)}
+        O_BACKS = {3: (0, 1), 4: (2, 3), 5: (4, 5), 6: (6, 7)}
         JOBS = [[("O", 1), ("O", 2)], [("O", 3)], [("O", 4), ("O", 5)], [("O", 6)], [("O", 7)], [], [], []]
         halves = (slice(0, HALF), slice(HALF, TOKENS))
         spread_bias()
@@ -487,26 +502,29 @@ def tile_customlstmcell_kernel(
                 blend_factor(step - UNITS)
         back("Z", 0)
         back("Z", 1)
+        SCALAR_JOBS = {4: ((reciprocal, 0), (reciprocal, 1)), 5: ((reciprocal, 2), (reciprocal, 3)), 6: ((reciprocal, 4), (reciprocal, 5)), 7: ((hidden_copy, 0), (reciprocal, 6), (hidden_copy, 1), (reciprocal, 7))}
         kept_cell(0)
         for step in range(UNITS):
             fresh_cell(step)
             kept_cell(step + 1)
+            for unit in DIVISORS.get(step, ()):
+                divisor(unit)
             cell(step)
-            divisor(step - 4)
+            for unit in NORMALISED.get(step, ()):
+                normalised_cell(unit)
             for unit in BLENDS[step]:
                 blend_factor(unit)
             for gate, k in JOBS[step]:
                 column_group(gate, k)
             back("Z", step + 2)
-            back("O", step - 3)
-            reciprocal(step - 4)
-        for step in range(UNITS + 2):
-            divisor(step + 4)
-            normalised_cell(step)
-            hidden(step - 1 if step > 2 else -1)
-            back("O", step + 5)
-            reciprocal(step + 4)
-            for unit in SUMS[step]:
+            for unit in O_BACKS.get(step, ()):
+                back("O", unit)
+            for unit in NORMALISED.get(step, ()):
                 hidden_sum(unit)
-            for unit in COPIES[step]:
+            for job, unit in SCALAR_JOBS.get(step, ()):
+                job(unit)
+        for step in range(3, UNITS + 1):
+            normalised_cell(step)
+            hidden(step - 1 if step > 3 else -1)
+            for unit in COPIES.get(step, ()):
                 hidden_copy(unit)

from contextlib import ExitStack

import concourse.mybir as mybir
from concourse.masks import make_identity

F32 = mybir.dt.float32
BF16 = mybir.dt.bfloat16
I32 = mybir.dt.int32
U32 = mybir.dt.uint32
U8 = mybir.dt.uint8
FP8X4 = mybir.dt.float8_e4m3fn_x4
ALU = mybir.AluOpType
ACT = mybir.ActivationFunctionType

P = 128
TOKENS = 512
TOKEN_TILES = TOKENS // P
HALF = TOKENS // 2
D = 512
DFF = 1024
K_PASS = 512
PASSES = (DFF + D) // K_PASS
CHUNK = 512
CHUNKS = DFF // CHUNK
UNITS = CHUNKS * TOKEN_TILES
COLUMN_TILES = DFF // P
TILES_PER_CHUNK = CHUNK // P
GATES = ("I", "F", "Z", "O")
FLIPPED = ("I", "Z", "O")
SMALLEST_NORMAL = 2.0 ** -126

FLOPS = 2 * TOKENS * (DFF + D) * 4 * DFF


def tile_customlstmcell_kernel(
    tc, Zi, Ci, Mi, Hi, Ni, m,
    WI_w_words, WI_w_scales, WI_b, WF_w_words, WF_w_scales, WF_b,
    WO_w_words, WO_w_scales, WO_b, WZ_w_words, WZ_w_scales, WZ_b,
    RI_w_words, RI_w_scales, RI_b, RF_w_words, RF_w_scales, RF_b,
    RO_w_words, RO_w_scales, RO_b, RZ_w_words, RZ_w_scales, RZ_b,
    out_0, out_1, out_2, out_3,
):
    nc = tc.nc
    w_words = {"I": WI_w_words, "F": WF_w_words, "Z": WZ_w_words, "O": WO_w_words}
    r_words = {"I": RI_w_words, "F": RF_w_words, "Z": RZ_w_words, "O": RO_w_words}
    w_scales = {"I": WI_w_scales, "F": WF_w_scales, "Z": WZ_w_scales, "O": WO_w_scales}
    r_scales = {"I": RI_w_scales, "F": RF_w_scales, "Z": RZ_w_scales, "O": RO_w_scales}
    w_bias = {"I": WI_b, "F": WF_b, "Z": WZ_b, "O": WO_b}
    r_bias = {"I": RI_b, "F": RF_b, "Z": RZ_b, "O": RO_b}

    def by_token(ap):
        return ap.flatten_outer_dims().rearrange("(p t) d -> p t d", t=TOKEN_TILES)

    c_out, m_out, h_out, n_out = by_token(out_0), by_token(out_1), by_token(out_2), by_token(out_3)

    with ExitStack() as ctx:
        keep = ctx.enter_context(tc.tile_pool(name="keep", bufs=1))
        columns = ctx.enter_context(tc.tile_pool(name="columns", bufs=2 * COLUMN_TILES))
        rotate = ctx.enter_context(tc.tile_pool(name="rotate", bufs=3))
        psum = ctx.enter_context(tc.psum_pool(name="psum", bufs=2))
        ctx.enter_context(tc.manual_schedule())

        hi_sb = keep.tile([P, TOKEN_TILES, DFF], BF16)
        zi_sb = keep.tile([P, TOKEN_TILES, D], BF16)
        mi_sb = keep.tile([P, TOKEN_TILES, DFF], BF16)
        ni_sb = keep.tile([P, TOKEN_TILES, DFF], BF16)
        ci_sb = keep.tile([P, TOKEN_TILES, DFF], BF16)
        codes = {}
        planes = {}
        for gate in GATES:
            gate_codes = keep.tile([P, PASSES, DFF], U32, align_bytes=64, name="codes_" + gate)
            codes[gate] = gate_codes
            gate_planes = keep.tile([P, DFF], U8, align_bytes=64, name="planes_" + gate)
            planes[gate] = gate_planes
        x_codes = keep.tile([P, PASSES, TOKENS], U32, align_bytes=64)
        x_scales = keep.tile([P, PASSES, TOKENS], U8, align_bytes=64)
        ident = keep.tile([P, P], F32)
        ident_bf = keep.tile([P, P], BF16)
        ones = keep.tile([P, P], BF16)
        idle_rows = keep.tile([P, CHUNK], BF16)
        bias_rows = keep.tile([P, DFF], BF16)
        minus_m = keep.tile([P, TOKEN_TILES, P], BF16)
        bias_f = keep.tile([P, DFF], F32)
        w_rows, r_rows, sum_rows = {}, {}, {}
        for name in ("I", "ZO"):
            w_tile = keep.tile([P, P], BF16, name="w_rows_" + name)
            r_tile = keep.tile([P, P], BF16, name="r_rows_" + name)
            sum_tile = keep.tile([P, P], F32, name="sum_rows_" + name)
            w_rows[name], r_rows[name], sum_rows[name] = w_tile, r_tile, sum_tile
        column_bias = keep.tile([P, len(FLIPPED), COLUMN_TILES], F32)
        m_bf = keep.tile([P, TOKEN_TILES], BF16)
        m_f32 = keep.tile([P, TOKEN_TILES], F32)
        m_floor = keep.tile([P, TOKEN_TILES], F32)
        one_minus_m = keep.tile([P, TOKEN_TILES], F32)
        f_pre = keep.tile([P, UNITS, CHUNK], F32)
        e_i = keep.tile([P, UNITS, CHUNK], F32)
        g = keep.tile([P, UNITS, CHUNK], F32)
        n_t = keep.tile([P, UNITS, CHUNK], F32)
        grouped = []
        for k in range(2 * PASSES):
            grouped_k = keep.tile([P, HALF * 4], BF16, align_bytes=64, name="grouped%d" % k)
            grouped.append(grouped_k)

        make_identity(nc, ident[:])
        nc.vector.memset(bias_rows[:].bitcast(I32), 0)
        nc.vector.memset(planes["F"][:].bitcast(I32), 0)
        nc.vector.memset(ones[:], 1.0)
        nc.vector.memset(idle_rows[:].bitcast(I32), 0)
        nc.vector.memset(w_rows["I"][:], 0.0)
        nc.vector.memset(r_rows["I"][:], 0.0)
        for gate in ("I", "Z", "O"):
            nc.vector.memset(planes[gate][:].bitcast(I32), 0)
        nc.vector.memset(w_rows["ZO"][:], 0.0)
        nc.vector.memset(r_rows["ZO"][:], 0.0)
        nc.vector.tensor_copy(out=ident_bf[:], in_=ident[:])

        def place(unit):
            chunk, t = divmod(unit, TOKEN_TILES)
            return t, slice(chunk * CHUNK, (chunk + 1) * CHUNK)

        def load_codes(gate, chunk):
            cols = slice(chunk * CHUNK, (chunk + 1) * CHUNK)
            nc.sync.dma_start(
                out=codes[gate][:, 0:2, cols].bitcast(I32),
                in_=w_words[gate].rearrange("g p n t -> p g (n t)").bitcast(I32)[:, :, cols],
            )
            nc.sync.dma_start(
                out=codes[gate][:, 2:3, cols].bitcast(I32),
                in_=r_words[gate].rearrange("g p n t -> p g (n t)").bitcast(I32)[:, :, cols],
            )

        def load_scales(gate, quadrants=(0, 1, 2, 3)):
            for q in quadrants:
                rows = slice(4 * q, 4 * q + 4)
                nc.sync.dma_start(
                    out=planes[gate][32 * q : 32 * q + 8, :].bitcast(I32),
                    in_=w_scales[gate][:, rows, :].bitcast(I32),
                )
                nc.sync.dma_start(
                    out=planes[gate][32 * q + 8 : 32 * q + 12, :].bitcast(I32),
                    in_=r_scales[gate][0, rows, :].bitcast(I32),
                )

        def load_column_biases(queue, name):
            for i, gate in enumerate(name):
                rows = slice(i * COLUMN_TILES, (i + 1) * COLUMN_TILES)
                queue.dma_start(out=w_rows[name][rows, :], in_=w_bias[gate].rearrange("(i n) -> i n", n=P))
                queue.dma_start(out=r_rows[name][rows, :], in_=r_bias[gate].rearrange("(i n) -> i n", n=P))

        def load_x(half, queue):
            tiles = slice(2 * half, 2 * half + 2)
            queue.dma_start(out=hi_sb[:, tiles, :], in_=by_token(Hi)[:, tiles, :])
            queue.dma_start(out=zi_sb[:, tiles, :], in_=by_token(Zi)[:, tiles, :])

        nc.gpsimd.dma_start(out=bias_rows[0:1, :], in_=w_bias["F"].unsqueeze(0))
        nc.gpsimd.dma_start(out=bias_rows[1:2, :], in_=r_bias["F"].unsqueeze(0))
        nc.gpsimd.dma_start(
            out=m_bf[:], in_=m.flatten_outer_dims().rearrange("(p t) o -> p (t o)", t=TOKEN_TILES)
        )
        load_x(0, nc.sync)
        nc.sync.dma_start(out=mi_sb[:, :, 0:CHUNK], in_=by_token(Mi)[:, :, 0:CHUNK])
        load_scales("F")
        load_codes("F", 0)
        load_column_biases(nc.sync, "I")
        load_x(1, nc.sync)
        load_scales("I")
        load_codes("I", 0)
        nc.sync.dma_start(out=mi_sb[:, :, CHUNK:DFF], in_=by_token(Mi)[:, :, CHUNK:DFF])
        load_codes("F", 1)
        load_codes("I", 1)
        nc.sync.dma_start(out=ni_sb[:], in_=by_token(Ni))
        load_scales("Z")
        load_codes("Z", 0)
        load_codes("Z", 1)
        load_column_biases(nc.gpsimd, "ZO")
        nc.sync.dma_start(out=ci_sb[:], in_=by_token(Ci))
        load_scales("O")
        load_codes("O", 0)
        load_codes("O", 1)

        x_blocks = ((hi_sb, 0), (hi_sb, 1), (zi_sb, 0))

        def warm_up(count):
            acc = psum.tile([P, CHUNK], F32, tag="group", bufs=3)
            for k in range(count):
                nc.tensor.matmul(out=acc[:], lhsT=ones[:], rhs=idle_rows[:], start=True, stop=True)

        def transpose_piece(half, c):
            x_sb, group = x_blocks[c]
            piece = half * PASSES + c
            x_words = x_sb[:].bitcast(F32)
            out_words = grouped[piece][:].bitcast(F32).rearrange("p (r u) -> p r u", u=2)
            xt = psum.tile([P, 2, 2 * P], F32, tag=("group" if half else "back"), bufs=3)
            for u in range(2):
                for s in range(2):
                    nc.tensor.transpose(
                        xt[:, u, s * P : (s + 1) * P],
                        x_words[:, 2 * half + s, 256 * group + u : 256 * (group + 1) : 2],
                        ident[:],
                    )
            copy = nc.vector.tensor_copy if piece in (0, 2) else nc.scalar.copy
            copy(out=out_words, in_=xt[:].rearrange("p u r -> p r u"))

        def quantise_piece(half, c):
            tokens = slice(half * HALF, (half + 1) * HALF)
            nc.vector.quantize_mx(
                out=x_codes[:, c, tokens].bitcast(FP8X4), scales=x_scales[:, c, tokens],
                in_=grouped[half * PASSES + c][:],
            )

        def sum_biases(name):
            nc.gpsimd.tensor_tensor(out=sum_rows[name][:], in0=w_rows[name][:], in1=r_rows[name][:], op=ALU.add)

        def flip_biases(name):
            flipped = psum.tile([P, P], F32, tag="back", bufs=3)
            nc.tensor.transpose(flipped[:], sum_rows[name][:], ident[:])
            return flipped

        def finish_biases(name, flipped):
            for i, gate in enumerate(name):
                nc.scalar.activation(
                    out=column_bias[:, FLIPPED.index(gate), :],
                    in_=flipped[:, i * COLUMN_TILES : (i + 1) * COLUMN_TILES],
                    func=ACT.Copy, scale=(-1.0 if gate == "O" else 1.0),
                )

        warm_up(3)
        for c in range(PASSES):
            transpose_piece(0, c)
        warm_up(4)
        for c in range(PASSES):
            quantise_piece(0, c)

        column_tiles = {}
        live = {}

        def valid(unit):
            return 0 <= unit < UNITS

        def prepare_m():
            nc.gpsimd.tensor_copy(out=m_f32[:], in_=m_bf[:])
            nc.gpsimd.tensor_scalar(out=m_floor[:], in0=m_bf[:], scalar1=SMALLEST_NORMAL, scalar2=None, op0=ALU.max)
            nc.gpsimd.tensor_scalar(
                out=one_minus_m[:], in0=m_bf[:], scalar1=-1.0, scalar2=1.0, op0=ALU.mult, op1=ALU.add
            )

        def column_group(gate, column_tile, tokens=slice(0, TOKENS)):
            cols = slice(column_tile * P, (column_tile + 1) * P)
            acc = psum.tile([P, TOKENS], F32, tag="group", bufs=3)
            for c in range(PASSES):
                nc.tensor.matmul_mx(
                    out=acc[:, tokens],
                    lhsT=codes[gate][:, c, cols].bitcast(FP8X4),
                    lhsT_scale=planes[gate][4 * c : P, cols],
                    rhs=x_codes[:, c, tokens].bitcast(FP8X4),
                    rhs_scale=x_scales[:, c, tokens],
                    start=(c == 0),
                    stop=(c == PASSES - 1),
                )
            if (gate, column_tile) not in column_tiles:
                by_column = columns.tile([P, TOKENS], F32, tag="column")
                column_tiles[gate, column_tile] = by_column
            i = FLIPPED.index(gate)
            nc.scalar.activation(
                out=column_tiles[gate, column_tile][:, tokens], in_=acc[:, tokens],
                func={"I": ACT.Identity, "Z": ACT.Tanh, "O": ACT.Exp}[gate],
                bias=column_bias[:, i, column_tile : column_tile + 1], scale=(-1.0 if gate == "O" else 1.0),
            )

        def back(gate, unit):
            if not valid(unit):
                return
            chunk, t = divmod(unit, TOKEN_TILES)
            by_token_ps = psum.tile([P, CHUNK], F32, tag=("f" if gate == "O" else "back"), bufs=(2 if gate == "O" else 3))
            for k in range(TILES_PER_CHUNK):
                nc.tensor.transpose(
                    by_token_ps[:, k * P : (k + 1) * P],
                    column_tiles[gate, chunk * TILES_PER_CHUNK + k][:, t * P : (t + 1) * P],
                    ident[:],
                )
            live[gate, unit] = by_token_ps

        def spread_bias():
            for chunk in range(CHUNKS):
                cols = slice(chunk * CHUNK, (chunk + 1) * CHUNK)
                acc = psum.tile([P, CHUNK], F32, tag="group", bufs=3)
                nc.tensor.matmul(out=acc[:], lhsT=ones[:], rhs=bias_rows[:, cols], start=True, stop=True)
                nc.scalar.copy(out=bias_f[:, cols], in_=acc[:])

        def early_stabiliser_bias(unit):
            t, cols = place(unit)
            engine = nc.vector if unit < TOKEN_TILES else nc.gpsimd
            engine.tensor_tensor(out=f_pre[:, unit, :], in0=mi_sb[:, t, cols], in1=bias_f[:, cols], op=ALU.add)

        def forget_matmuls(unit):
            if not valid(unit):
                return
            t, cols = place(unit)
            tokens = slice(t * P, (t + 1) * P)
            acc = psum.tile([P, CHUNK], F32, tag="f")
            for c in range(PASSES):
                nc.tensor.matmul_mx(
                    out=acc[:],
                    lhsT=x_codes[:, c, tokens].bitcast(FP8X4),
                    lhsT_scale=x_scales[:, c, tokens],
                    rhs=codes["F"][:, c, cols].bitcast(FP8X4),
                    rhs_scale=planes["F"][4 * c : P, cols],
                    start=(c == 0),
                    stop=(c == PASSES - 1),
                )
            live["F", unit] = acc

        def forget_gate(unit):
            if valid(unit):
                nc.vector.tensor_tensor(
                    out=f_pre[:, unit, :], in0=live["F", unit][:], in1=f_pre[:, unit, :], op=ALU.add
                )

        def difference(unit):
            if valid(unit):
                d = rotate.tile([P, CHUNK], F32, tag="d")
                nc.vector.tensor_tensor(out=d[:], in0=f_pre[:, unit, :], in1=live["I", unit][:], op=ALU.subtract)
                live["d", unit] = d

        def stabiliser(unit):
            if valid(unit):
                t, cols = place(unit)
                nc.vector.tensor_tensor(
                    out=f_pre[:, unit, :], in0=f_pre[:, unit, :], in1=live["I", unit][:], op=ALU.max
                )
                nc.sync.dma_start(out=m_out[:, t, cols], in_=f_pre[:, unit, :])

        def exponentials(unit):
            if valid(unit):
                d = live["d", unit]
                nc.scalar.activation(out=g[:, unit, :], in_=d[:], func=ACT.Exp)
                nc.scalar.activation(out=e_i[:, unit, :], in_=d[:], func=ACT.Exp, scale=-1.0)

        def blend_factor(unit):
            if valid(unit):
                t, cols = place(unit)
                nc.scalar.activation(
                    out=g[:, unit, :], in_=g[:, unit, :], func=ACT.Identity,
                    scale=m_floor[:, t : t + 1], bias=one_minus_m[:, t : t + 1],
                )

        def forgotten_n(unit):
            if valid(unit):
                t, cols = place(unit)
                nc.vector.scalar_tensor_tensor(
                    out=n_t[:, unit, :], in0=g[:, unit, :], scalar=1.0, in1=ni_sb[:, t, cols],
                    op0=ALU.min, op1=ALU.mult,
                )

        def normaliser(unit):
            if valid(unit):
                t, cols = place(unit)
                nc.vector.scalar_tensor_tensor(
                    out=n_t[:, unit, :], in0=e_i[:, unit, :], scalar=1.0, in1=n_t[:, unit, :],
                    op0=ALU.min, op1=ALU.add,
                )
                nc.sync.dma_start(out=n_out[:, t, cols], in_=n_t[:, unit, :])

        def kept_cell(unit):
            if valid(unit):
                t, cols = place(unit)
                nc.vector.scalar_tensor_tensor(
                    out=g[:, unit, :], in0=g[:, unit, :], scalar=1.0, in1=ci_sb[:, t, cols],
                    op0=ALU.min, op1=ALU.mult,
                )

        def fresh_cell(unit):
            if valid(unit):
                nc.vector.scalar_tensor_tensor(
                    out=e_i[:, unit, :], in0=e_i[:, unit, :], scalar=1.0, in1=live["Z", unit][:],
                    op0=ALU.min, op1=ALU.mult,
                )

        def cell(unit):
            if valid(unit):
                t, cols = place(unit)
                nc.vector.scalar_tensor_tensor(
                    out=g[:, unit, :], in0=e_i[:, unit, :], scalar=m_f32[:, t : t + 1], in1=g[:, unit, :],
                    op0=ALU.mult, op1=ALU.add,
                )
                nc.sync.dma_start(out=c_out[:, t, cols], in_=g[:, unit, :])

        def divisor(unit):
            if valid(unit):
                nc.vector.scalar_tensor_tensor(
                    out=n_t[:, unit, :], in0=live["O", unit][:], scalar=1.0, in1=n_t[:, unit, :],
                    op0=ALU.add, op1=ALU.mult,
                )

        def reciprocal(unit):
            if valid(unit):
                nc.scalar.activation(out=n_t[:, unit, :], in_=n_t[:, unit, :], func=ACT.Abs_reciprocal_sqrt)
                nc.scalar.activation(out=n_t[:, unit, :], in_=n_t[:, unit, :], func=ACT.Square)

        def normalised_cell(unit):
            if valid(unit):
                t, cols = place(unit)
                nc.vector.scalar_tensor_tensor(
                    out=n_t[:, unit, :], in0=g[:, unit, :], scalar=m_f32[:, t : t + 1], in1=n_t[:, unit, :],
                    op0=ALU.mult, op1=ALU.mult,
                )

        def prepare_blend():
            for t in range(TOKEN_TILES):
                nc.gpsimd.tensor_scalar(
                    out=minus_m[:, t, :], in0=ident_bf[:], scalar1=m_f32[:, t : t + 1], scalar2=-1.0,
                    op0=ALU.mult, op1=ALU.mult,
                )

        def hidden_sum(unit):
            t, cols = place(unit)
            acc = psum.tile([P, CHUNK], F32, tag="group", bufs=3)
            nc.tensor.matmul(out=acc[:], lhsT=ident_bf[:], rhs=hi_sb[:, t, cols], start=True, stop=False)
            nc.tensor.matmul(out=acc[:], lhsT=minus_m[:, t, :], rhs=hi_sb[:, t, cols], start=False, stop=False)
            nc.tensor.matmul(out=acc[:], lhsT=ident[:], rhs=n_t[:, unit, :], start=False, stop=True)
            live["H", unit] = acc

        def hidden_copy(unit):
            t, cols = place(unit)
            nc.scalar.copy(out=n_t[:, unit, :], in_=live["H", unit][:])
            nc.sync.dma_start(out=h_out[:, t, cols], in_=n_t[:, unit, :])

        def hidden(unit):
            if valid(unit):
                t, cols = place(unit)
                parts = 2 if unit == UNITS - 1 else 1
                width = CHUNK // parts
                for part in range(parts):
                    own = slice(part * width, (part + 1) * width)
                    cols = slice(unit // TOKEN_TILES * CHUNK + part * width, unit // TOKEN_TILES * CHUNK + (part + 1) * width)
                    nc.vector.scalar_tensor_tensor(
                        out=n_t[:, unit, own], in0=hi_sb[:, t, cols], scalar=one_minus_m[:, t : t + 1],
                        in1=n_t[:, unit, own], op0=ALU.mult, op1=ALU.add,
                    )
                    nc.sync.dma_start(out=h_out[:, t, cols], in_=n_t[:, unit, own])

        A_JOBS = {0: (("I", 4),), 1: (("I", 5),), 2: (("I", 6), ("I", 7)), 4: (("Z", 0), ("Z", 1)), 5: (("Z", 2),), 6: (("Z", 3), ("Z", 4)), 7: (("Z", 5),), 8: (("Z", 6), ("Z", 7)), 9: (("O", 0),)}
        I_BACKS = {0: (2,), 1: (3,), 2: (4,), 3: (5,), 4: (6,), 5: (7,)}
        BLENDS = [[2, 3], [4], [5, 6], [7], [], [], [], []]
        COPIES = {4: (2,)}
        NORMALISED = {6: (0, 1), 7: (2,)}
        DIVISORS = {4: (0, 1), 5: (2, 3), 6: (4, 5), 7: (6, 7)}
        O_BACKS = {3: (0, 1), 4: (2, 3), 5: (4, 5), 6: (6, 7)}
        JOBS = [[("O", 1), ("O", 2)], [("O", 3)], [("O", 4), ("O", 5)], [("O", 6)], [("O", 7)], [], [], []]
        halves = (slice(0, HALF), slice(HALF, TOKENS))
        spread_bias()
        for unit in range(TOKEN_TILES):
            early_stabiliser_bias(unit)
        for unit in range(2):
            forget_matmuls(unit)
            forget_gate(unit)
        for c in range(PASSES):
            transpose_piece(1, c)
        sum_biases("I")
        flipped_i = flip_biases("I")
        quantise_piece(1, 0)
        finish_biases("I", flipped_i)
        quantise_piece(1, 1)
        quantise_piece(1, 2)
        prepare_m()
        for unit in range(TOKEN_TILES, UNITS):
            early_stabiliser_bias(unit)
        sum_biases("ZO")
        for unit in (2, 3):
            forget_matmuls(unit)
            forget_gate(unit)
        for k in range(TILES_PER_CHUNK):
            column_group("I", k, halves[0])
        back("I", 0)
        back("I", 1)
        column_group("I", 0, halves[1])
        column_group("I", 1, halves[1])
        column_group("I", 2, halves[1])
        column_group("I", 3, halves[1])
        for step in range(UNITS + 2):
            forgotten_n(step - 2)
            difference(step)
            normaliser(step - 2)
            stabiliser(step)
            forget_gate(step + 3 if step >= 1 else -1)
            if step == 2:
                flipped_zo = flip_biases("ZO")
            if step == 3:
                finish_biases("ZO", flipped_zo)
                prepare_blend()
            if step < 1:
                exponentials(step)
                forget_matmuls(step + 4)
            for gate, k in A_JOBS.get(step, ()):
                column_group(gate, k)
            if step >= 1:
                exponentials(step)
                forget_matmuls(step + 4)
            for unit in I_BACKS.get(step, ()):
                back("I", unit)
            if step >= UNITS:
                blend_factor(step - UNITS)
        back("Z", 0)
        back("Z", 1)
        SCALAR_JOBS = {4: ((reciprocal, 0), (reciprocal, 1)), 5: ((reciprocal, 2), (reciprocal, 3)), 6: ((reciprocal, 4), (reciprocal, 5)), 7: ((hidden_copy, 0), (reciprocal, 6), (hidden_copy, 1), (reciprocal, 7))}
        kept_cell(0)
        for step in range(UNITS):
            fresh_cell(step)
            kept_cell(step + 1)
            for unit in DIVISORS.get(step, ()):
                divisor(unit)
            cell(step)
            for unit in NORMALISED.get(step, ()):
                normalised_cell(unit)
            for unit in BLENDS[step]:
                blend_factor(unit)
            for gate, k in JOBS[step]:
                column_group(gate, k)
            back("Z", step + 2)
            for unit in O_BACKS.get(step, ()):
                back("O", unit)
            for unit in NORMALISED.get(step, ()):
                hidden_sum(unit)
            for job, unit in SCALAR_JOBS.get(step, ()):
                job(unit)
        for step in range(3, UNITS + 1):
            normalised_cell(step)
            hidden(step - 1 if step > 3 else -1)
            for unit in COPIES.get(step, ()):
                hidden_copy(unit)
